import numpy as np
import ml_dtypes


def mxq(x, axis, fmt="e4m3"):
    dtype, down = {"e4m3": (ml_dtypes.float8_e4m3fn, 7), "e5m2": (ml_dtypes.float8_e5m2, 14)}[fmt]
    v = np.moveaxis(np.asarray(x, np.float32).astype(ml_dtypes.bfloat16).astype(np.float64), axis, -1)
    blocks = v.reshape(v.shape[:-1] + (-1, 32))
    amax = np.abs(blocks).max(-1, keepdims=True)
    byte = np.maximum(np.where(amax > 0, np.frexp(amax)[1] - 1 + 127, 0) - down, 1)
    scale = np.exp2(byte - 127.0)
    codes = (blocks / scale).astype(np.float32).astype(dtype).astype(np.float64)
    return np.moveaxis((codes * scale).reshape(v.shape), -1, axis)


WIDE = False


def mx_kscale(k):
    if not WIDE:
        return np.ones(k)
    levels = np.array([10, -10, 5, -5, 0])
    a = np.random.permutation(np.resize(levels, k // 512 * 4)).reshape(k // 512, 4)
    idx = np.arange(k)
    return np.exp2(a[idx // 512, idx % 128 // 32])


BF16 = ml_dtypes.bfloat16


def bf(x):
    return np.asarray(x, np.float32).astype(BF16)


def f64(x):
    return np.asarray(x).astype(np.float64)


M, I, O = 1024, 2048, 2048
SPARSITY = 0.98


def _build_mask():
    num_connections = int((1 - SPARSITY) * I * O)
    cpn = max(1, num_connections // O)
    rows = np.arange(O)[:, None]
    cols = (rows * cpn + np.arange(cpn)[None, :]) % I
    mask = np.zeros((O, I), dtype=np.float32)
    mask[np.repeat(np.arange(O), cpn), cols.reshape(-1)] = 1.0
    return mask, cpn


def setup_inputs():
    s = mx_kscale(I)
    mask_np, cpn = _build_mask()
    return {"x": bf(np.random.standard_normal((M, I)) * s),
            "weight": bf(np.random.standard_normal((O, I)) * np.sqrt(2.0 / cpn) / s[None, :]),
            "bias": bf(np.random.standard_normal(O) * 0.1),
            "mask": bf(mask_np)}


def reference(x, weight, bias, mask):
    masked_weight = f64(weight) * f64(mask)
    return (mxq(f64(x), 1, "e4m3") @ mxq(masked_weight, 1, "e4m3").T) + f64(bias)

@@ -1,0 +1,264 @@
+from contextlib import ExitStack
+
+import concourse.mybir as mybir
+from concourse.masks import make_identity
+
+F32 = mybir.dt.float32
+BF16 = mybir.dt.bfloat16
+U32 = mybir.dt.uint32
+U8 = mybir.dt.uint8
+I32 = mybir.dt.int32
+FP8X4 = mybir.dt.float8_e4m3fn_x4
+ADD = mybir.AluOpType.add
+MULT = mybir.AluOpType.mult
+
+P = 128
+M, K, O = 1024, 2048, 2048
+MT = M // P
+FLOPS = 2 * M * O * 64
+BYTES = M * K * 2 + M * O * 4 + 2 * O * 64 * 2 + O * 2
+
+FRONT = 32
+S = 576
+L = 120
+LP = 128
+DIAG = S + 40
+ROWSTEP = K + 40
+CELL0 = FRONT - 24
+SCALAR_TILES = (1, 3, 5)
+
+
+def tile_structuredconnection_kernel(tc, x, weight, bias, mask, out):
+    nc = tc.nc
+    with ExitStack() as ctx:
+        keep = ctx.enter_context(tc.tile_pool(name="keep", bufs=1))
+        xgp = ctx.enter_context(tc.tile_pool(name="xgp", bufs=3))
+        outp = ctx.enter_context(tc.tile_pool(name="outp", bufs=4))
+        tp = ctx.enter_context(tc.psum_pool(name="tp", bufs=3))
+        accp = ctx.enter_context(tc.psum_pool(name="accp", bufs=5))
+
+        wa = keep.tile([P, 13, LP], BF16)
+        ma = keep.tile([P, 13, LP], BF16)
+        wb = keep.tile([P, 12, LP], BF16)
+        mb = keep.tile([P, 12, LP], BF16)
+        wp = keep.tile([P, 64], BF16)
+        mp = keep.tile([P, 64], BF16)
+        za = keep.tile([P, CELL0 + 13 * DIAG], BF16, align_bytes=64)
+        zb = keep.tile([P, CELL0 + 12 * DIAG], BF16, align_bytes=64)
+        g = keep.tile([P, 8192], BF16, align_bytes=64)
+        gs = keep.tile([P, 2048], BF16, align_bytes=64)
+        wq = keep.tile([P, 2048], U32, align_bytes=64)
+        ws = keep.tile([P, 2048], U8, align_bytes=64)
+        wsq = keep.tile([P, 512], U32, align_bytes=64)
+        wss = keep.tile([P, 512], U8, align_bytes=64)
+        x_sb = keep.tile([P, MT * K], BF16, align_bytes=64)
+        xq = keep.tile([P, MT * 512], U32, align_bytes=64)
+        xs = keep.tile([P, MT * 512], U8, align_bytes=64)
+        ident = keep.tile([P, P], F32)
+        ones = keep.tile([P, P], BF16)
+        bz = keep.tile([P, O], BF16)
+        bias_bc = keep.tile([P, O + 256], F32)
+
+        nc.vector.memset(wa[0:32, 0, 0:32], 0.0)
+        nc.vector.memset(ma[0:32, 0, 0:32], 0.0)
+        nc.vector.memset(wb[0:32, 11, 96:LP], 0.0)
+        nc.vector.memset(mb[0:32, 11, 96:LP], 0.0)
+        make_identity(nc, ident[:])
+
+        wj = weight.rearrange("(j r) k -> j (r k)", j=8)
+        mj = mask.rearrange("(j r) k -> j (r k)", j=8)
+
+        def cells(src, base, c, a0, a1, i0, i1):
+            s0 = (base + a0) * K + 512 * c + 40 * a0 - 24
+            n = a1 - a0
+            if n == 1:
+                return src[:, s0 + i0 : s0 + i1]
+            assert s0 >= 0 and s0 + n * ROWSTEP <= 256 * K
+            return src[:, s0 : s0 + n * ROWSTEP].rearrange("j (a w) -> j a w", w=ROWSTEP)[:, :, i0:i1]
+
+        def load(queue, src, dst, p0, base, c, a0, a1, i0, i1):
+            if a1 - a0 == 1:
+                queue.dma_start(out=dst[p0 : p0 + 8, a0, i0:i1], in_=cells(src, base, c, a0, a1, i0, i1))
+            else:
+                queue.dma_start(out=dst[p0 : p0 + 8, a0:a1, i0:i1], in_=cells(src, base, c, a0, a1, i0, i1))
+
+        for queue, src, dst_a, dst_b, dst_p in ((nc.sync, wj, wa, wb, wp), (nc.scalar, mj, ma, mb, mp)):
+            for c in range(4):
+                base = 64 * c + 52
+                if c == 3:
+                    load(queue, src, dst_b, 8 * c, base, c, 0, 11, 0, L)
+                    load(queue, src, dst_b, 8 * c, base, c, 11, 12, 0, 96)
+                else:
+                    load(queue, src, dst_b, 8 * c, base, c, 0, 12, 0, L)
+            for c in range(4):
+                for vp in range(4):
+                    v = 3 - vp
+                    base = 64 * ((c - v) % 4) + 13 * v
+                    p0 = 8 * (4 * c + vp)
+                    if c == 0 and v == 0:
+                        load(queue, src, dst_a, p0, base, c, 1, 13, 0, L)
+                        load(queue, src, dst_a, p0, base, c, 0, 1, 24, L)
+                    else:
+                        load(queue, src, dst_a, p0, base, c, 0, 13, 0, L)
+                    if c == 3:
+                        r0 = (base + 12) * K
+                        queue.dma_start(out=dst_p[p0 : p0 + 8, :], in_=src[:, r0 : r0 + 64])
+
+        for mt in range(MT):
+            nc.sync.dma_start(out=x_sb[:, mt * K : (mt + 1) * K], in_=x[mt * P : (mt + 1) * P, :])
+        nc.gpsimd.memset(bz[:].bitcast(F32), 0.0)
+        nc.scalar.dma_start(out=bz[0:1, :], in_=bias.rearrange("(o n) -> o n", o=1))
+
+        nc.gpsimd.memset(ones[:], 1.0)
+        nc.vector.memset(za[:].bitcast(I32)[:, 0 : (FRONT + 12 * S + 768) // 2], 0)
+        nc.gpsimd.memset(zb[:].bitcast(F32)[:, 0 : (CELL0 + 11 * DIAG + L) // 2], 0.0)
+        nc.vector.memset(gs[:].bitcast(I32), 0)
+
+        for n in range(4):
+            bps = accp.tile([P, 512], F32, tag="acc")
+            nc.tensor.matmul(bps[:], lhsT=ones[:], rhs=bz[:, 512 * n : 512 * n + 512], start=True, stop=True)
+            nc.scalar.copy(out=bias_bc[:, 512 * n : 512 * n + 512], in_=bps[:])
+
+        za_cells = za[:, CELL0 : CELL0 + 13 * DIAG].rearrange("p (a w) -> p a w", w=DIAG)
+        zb_cells = zb[:, CELL0 : CELL0 + 12 * DIAG].rearrange("p (a w) -> p a w", w=DIAG)
+        nc.vector.tensor_tensor(out=zb_cells[0:32, :, 0:L], in0=wb[0:32, :, 0:L], in1=mb[0:32, :, 0:L], op=MULT)
+        nc.vector.tensor_tensor(out=za_cells[:, 12:13, 0:L], in0=wa[:, 12:13, 0:L], in1=ma[:, 12:13, 0:L], op=MULT)
+        spill0 = FRONT + 12 * S + 512
+        nc.vector.tensor_tensor(out=za[96:128, spill0 : spill0 + 64], in0=wp[96:128, :], in1=mp[96:128, :], op=MULT)
+        for a0 in (0, 4, 8):
+            nc.vector.tensor_tensor(
+                out=za_cells[:, a0 : a0 + 4, 0:L], in0=wa[:, a0 : a0 + 4, 0:L], in1=ma[:, a0 : a0 + 4, 0:L], op=MULT
+            )
+
+        zaf = za[:].bitcast(F32)
+        zbf = zb[:].bitcast(F32)
+        gf = g[:].bitcast(F32).rearrange("p (q c n u) -> p q c n u", q=4, c=4, u=2)
+        gsf = gs[:].bitcast(F32).rearrange("p (c n u) -> p c n u", c=4, u=2)
+
+        def strip(pt, slot, zf, a):
+            for uh in range(2):
+                w0 = (FRONT + S * a + 256 * uh) // 2
+                nc.tensor.transpose(pt[:, 2 * slot + uh, :], zf[:, w0 : w0 + P], ident[:])
+
+        def quantise_w(q):
+            nc.vector.quantize_mx(
+                out=wq[:, 512 * q : 512 * q + 512].bitcast(FP8X4),
+                scales=ws[:, 512 * q : 512 * q + 512],
+                in_=g[:, 2048 * q : 2048 * q + 2048],
+            )
+
+        for a0 in range(0, 12, 2):
+            pt = tp.tile([P, 4, P], F32, tag="pt")
+            for slot in range(2):
+                a = a0 + slot
+                strip(pt, slot, zbf, a)
+                nc.scalar.copy(
+                    out=gf[:, 3, :, 32 + 8 * a : 40 + 8 * a, :],
+                    in_=pt[:, 2 * slot : 2 * slot + 2, 0:32].rearrange("p u (c n) -> p c n u", c=4),
+                )
+        pt = tp.tile([P, 4, P], F32, tag="pt")
+        strip(pt, 0, zaf, 12)
+        w0 = spill0 // 2
+        nc.tensor.transpose(pt[:, 2, :], zaf[:, w0 : w0 + P], ident[:])
+        nc.scalar.copy(out=gf[:, 3, :, 0:32, :], in_=pt[:, 0:2, :].rearrange("p u (c n) -> p c n u", c=4))
+        nc.scalar.copy(out=gsf[:, :, 0:32, 0], in_=pt[:, 2, :].rearrange("p (c n) -> p c n", c=4))
+        quantise_w(3)
+        nc.vector.quantize_mx(out=wsq[:].bitcast(FP8X4), scales=wss[:], in_=gs[:])
+        for a0 in range(0, 12, 2):
+            pt = tp.tile([P, 4, P], F32, tag="pt")
+            for slot in range(2):
+                a = a0 + slot
+                strip(pt, slot, zaf, a)
+                dst = gf[:, a // 4, :, 32 * (a % 4) : 32 * (a % 4) + 32, :]
+                src = pt[:, 2 * slot : 2 * slot + 2, :].rearrange("p u (c n) -> p c n u", c=4)
+                nc.scalar.copy(out=dst, in_=src)
+            if a0 % 4 == 2:
+                quantise_w(a0 // 4)
+
+        xf = x_sb[:].bitcast(F32)
+
+        def prepare_x(mt):
+            xg = xgp.tile([P, 2048], BF16, align_bytes=64, tag="xg")
+            xgf = xg[:].bitcast(F32).rearrange("p (c m u) -> p c m u", c=4, u=2)
+            for h in range(2):
+                pt = tp.tile([P, 4, P], F32, tag="pt")
+                for k in range(4):
+                    w0 = mt * 1024 + 512 * h + 128 * k
+                    nc.tensor.transpose(pt[:, k, :], xf[:, w0 : w0 + P], ident[:])
+                src = pt[:].rearrange("p (c u) m -> p c m u", c=2)
+                if h == 1 and mt < 2:
+                    nc.vector.tensor_copy(out=xgf[:, 2 * h : 2 * h + 2, :, :], in_=src)
+                else:
+                    nc.scalar.copy(out=xgf[:, 2 * h : 2 * h + 2, :, :], in_=src)
+            nc.vector.quantize_mx(
+                out=xq[:, 512 * mt : 512 * mt + 512].bitcast(FP8X4),
+                scales=xs[:, 512 * mt : 512 * mt + 512],
+                in_=xg[:],
+            )
+
+        def x_operand(mt, c):
+            lo = 512 * mt + 128 * c
+            return xq[:, lo : lo + 128].bitcast(FP8X4), xs[:, lo : lo + 128]
+
+        def runs(t, b0, nv, na):
+            v = t[:, b0 : b0 + 2048].rearrange("p (j r) -> p j r", r=256)[:, :, 0 : 51 * nv]
+            return v.rearrange("p j (v s) -> p j v s", s=51)[:, :, :, 0:na]
+
+        def multiply(mt):
+            by_scalar = mt in SCALAR_TILES
+            o_sb = outp.tile([P, O + 256], F32, tag="o_sb")
+            for c in range(4):
+                acc = accp.tile([P, 512], F32, tag="acc")
+                lhs, lhs_s = x_operand(mt, c)
+                for q in range(4):
+                    lo = 512 * q + 128 * c
+                    nc.tensor.matmul_mx(
+                        out=acc[:, 128 * q : 128 * q + 128],
+                        lhsT=lhs,
+                        lhsT_scale=lhs_s,
+                        rhs=wq[:, lo : lo + 128].bitcast(FP8X4),
+                        rhs_scale=ws[:, lo : lo + 128],
+                        start=True,
+                        stop=(q < 3),
+                    )
+                lhs, lhs_s = x_operand(mt, (c + 1) % 4)
+                nc.tensor.matmul_mx(
+                    out=acc[:, 384:512],
+                    lhsT=lhs,
+                    lhsT_scale=lhs_s,
+                    rhs=wsq[:, 128 * c : 128 * c + 128].bitcast(FP8X4),
+                    rhs_scale=wss[:, 128 * c : 128 * c + 128],
+                    start=False,
+                    stop=True,
+                )
+                pa = acc[:, 0:416].rearrange("p (a v j) -> p j v a", v=4, j=8)
+                for vp0, vp1, b0 in ((0, 3 - c, 64 * c + 103), (3 - c, 4, 64 * c - 153 + 51 * (3 - c))):
+                    nv = vp1 - vp0
+                    if nv > 0 and by_scalar:
+                        nc.scalar.copy(out=runs(o_sb, b0, nv, 13), in_=pa[:, :, vp0:vp1, :])
+                    elif nv > 0:
+                        nc.vector.tensor_tensor(
+                            out=runs(o_sb, b0, nv, 13), in0=pa[:, :, vp0:vp1, :], in1=runs(bias_bc, b0, nv, 13), op=ADD
+                        )
+                pb = acc[:, 416:512].rearrange("p (a j) -> p j a", j=8)
+                b0 = 64 * c + 52
+                o_run = o_sb[:, b0 : b0 + 2048].rearrange("p (j r) -> p j r", r=256)[:, :, 0:12]
+                if by_scalar:
+                    nc.scalar.copy(out=o_run, in_=pb)
+                else:
+                    nc.vector.tensor_tensor(
+                        out=o_run,
+                        in0=pb,
+                        in1=bias_bc[:, b0 : b0 + 2048].rearrange("p (j r) -> p j r", r=256)[:, :, 0:12],
+                        op=ADD,
+                    )
+            if by_scalar:
+                nc.gpsimd.tensor_tensor(out=o_sb[:, 0:O], in0=o_sb[:, 0:O], in1=bias_bc[:, 0:O], op=ADD)
+            nc.sync.dma_start(out=out[mt * P : (mt + 1) * P, :], in_=o_sb[:, 0:O])
+
+        prepare_x(0)
+        prepare_x(1)
+        for mt in range(MT):
+            if mt + 2 < MT:
+                prepare_x(mt + 2)
+            multiply(mt)

@@ -25,7 +25,7 @@ LP = 128
 DIAG = S + 40
 ROWSTEP = K + 40
 CELL0 = FRONT - 24
-SCALAR_TILES = (1, 3, 5)
+SCALAR_TILES = (1, 3, 5, 6)
 
 
 def tile_structuredconnection_kernel(tc, x, weight, bias, mask, out):
@@ -34,8 +34,8 @@ def tile_structuredconnection_kernel(tc, x, weight, bias, mask, out):
         keep = ctx.enter_context(tc.tile_pool(name="keep", bufs=1))
         xgp = ctx.enter_context(tc.tile_pool(name="xgp", bufs=3))
         outp = ctx.enter_context(tc.tile_pool(name="outp", bufs=4))
-        tp = ctx.enter_context(tc.psum_pool(name="tp", bufs=3))
-        accp = ctx.enter_context(tc.psum_pool(name="accp", bufs=5))
+        tp = ctx.enter_context(tc.psum_pool(name="tp", bufs=2))
+        accp = ctx.enter_context(tc.psum_pool(name="accp", bufs=6))
 
         wa = keep.tile([P, 13, LP], BF16)
         ma = keep.tile([P, 13, LP], BF16)
@@ -171,7 +171,10 @@ def tile_structuredconnection_kernel(tc, x, weight, bias, mask, out):
                 strip(pt, slot, zaf, a)
                 dst = gf[:, a // 4, :, 32 * (a % 4) : 32 * (a % 4) + 32, :]
                 src = pt[:, 2 * slot : 2 * slot + 2, :].rearrange("p u (c n) -> p c n u", c=4)
-                nc.scalar.copy(out=dst, in_=src)
+                if slot == 0:
+                    nc.scalar.copy(out=dst, in_=src)
+                else:
+                    nc.vector.tensor_copy(out=dst, in_=src)
             if a0 % 4 == 2:
                 quantise_w(a0 // 4)
 

@@ -25,7 +25,6 @@ LP = 128
 DIAG = S + 40
 ROWSTEP = K + 40
 CELL0 = FRONT - 24
-SCALAR_TILES = (1, 3, 5, 6)
 
 
 def tile_structuredconnection_kernel(tc, x, weight, bias, mask, out):
@@ -34,8 +33,8 @@ def tile_structuredconnection_kernel(tc, x, weight, bias, mask, out):
         keep = ctx.enter_context(tc.tile_pool(name="keep", bufs=1))
         xgp = ctx.enter_context(tc.tile_pool(name="xgp", bufs=3))
         outp = ctx.enter_context(tc.tile_pool(name="outp", bufs=4))
-        tp = ctx.enter_context(tc.psum_pool(name="tp", bufs=2))
-        accp = ctx.enter_context(tc.psum_pool(name="accp", bufs=6))
+        psum = ctx.enter_context(tc.psum_pool(name="psum", bufs=8))
+        ctx.enter_context(tc.manual_schedule())
 
         wa = keep.tile([P, 13, LP], BF16)
         ma = keep.tile([P, 13, LP], BF16)
@@ -82,30 +81,39 @@ def tile_structuredconnection_kernel(tc, x, weight, bias, mask, out):
             else:
                 queue.dma_start(out=dst[p0 : p0 + 8, a0:a1, i0:i1], in_=cells(src, base, c, a0, a1, i0, i1))
 
-        for queue, src, dst_a, dst_b, dst_p in ((nc.sync, wj, wa, wb, wp), (nc.scalar, mj, ma, mb, mp)):
+        def load_x(t0):
+            nc.sync.dma_start(
+                out=x_sb[:, t0 * K : (t0 + 2) * K].rearrange("p (t k) -> p t k", t=2),
+                in_=x[t0 * P : (t0 + 2) * P, :].rearrange("(t p) k -> p t k", p=P),
+            )
+
+        both = ((wj, wa, wb, wp), (mj, ma, mb, mp))
+        load_x(0)
+        for src, dst_a, dst_b, dst_p in both:
             for c in range(4):
                 base = 64 * c + 52
                 if c == 3:
-                    load(queue, src, dst_b, 8 * c, base, c, 0, 11, 0, L)
-                    load(queue, src, dst_b, 8 * c, base, c, 11, 12, 0, 96)
+                    load(nc.sync, src, dst_b, 8 * c, base, c, 0, 11, 0, L)
+                    load(nc.sync, src, dst_b, 8 * c, base, c, 11, 12, 0, 96)
                 else:
-                    load(queue, src, dst_b, 8 * c, base, c, 0, 12, 0, L)
+                    load(nc.sync, src, dst_b, 8 * c, base, c, 0, 12, 0, L)
+        load_x(2)
+        load_x(4)
+        load_x(6)
+        for src, dst_a, dst_b, dst_p in both:
             for c in range(4):
                 for vp in range(4):
                     v = 3 - vp
                     base = 64 * ((c - v) % 4) + 13 * v
                     p0 = 8 * (4 * c + vp)
                     if c == 0 and v == 0:
-                        load(queue, src, dst_a, p0, base, c, 1, 13, 0, L)
-                        load(queue, src, dst_a, p0, base, c, 0, 1, 24, L)
+                        load(nc.sync, src, dst_a, p0, base, c, 1, 13, 0, L)
+                        load(nc.sync, src, dst_a, p0, base, c, 0, 1, 24, L)
                     else:
-                        load(queue, src, dst_a, p0, base, c, 0, 13, 0, L)
+                        load(nc.sync, src, dst_a, p0, base, c, 0, 13, 0, L)
                     if c == 3:
                         r0 = (base + 12) * K
-                        queue.dma_start(out=dst_p[p0 : p0 + 8, :], in_=src[:, r0 : r0 + 64])
-
-        for mt in range(MT):
-            nc.sync.dma_start(out=x_sb[:, mt * K : (mt + 1) * K], in_=x[mt * P : (mt + 1) * P, :])
+                        nc.sync.dma_start(out=dst_p[p0 : p0 + 8, :], in_=src[:, r0 : r0 + 64])
         nc.gpsimd.memset(bz[:].bitcast(F32), 0.0)
         nc.scalar.dma_start(out=bz[0:1, :], in_=bias.rearrange("(o n) -> o n", o=1))
 
@@ -114,26 +122,20 @@ def tile_structuredconnection_kernel(tc, x, weight, bias, mask, out):
         nc.gpsimd.memset(zb[:].bitcast(F32)[:, 0 : (CELL0 + 11 * DIAG + L) // 2], 0.0)
         nc.vector.memset(gs[:].bitcast(I32), 0)
 
-        for n in range(4):
-            bps = accp.tile([P, 512], F32, tag="acc")
-            nc.tensor.matmul(bps[:], lhsT=ones[:], rhs=bz[:, 512 * n : 512 * n + 512], start=True, stop=True)
-            nc.scalar.copy(out=bias_bc[:, 512 * n : 512 * n + 512], in_=bps[:])
-
         za_cells = za[:, CELL0 : CELL0 + 13 * DIAG].rearrange("p (a w) -> p a w", w=DIAG)
         zb_cells = zb[:, CELL0 : CELL0 + 12 * DIAG].rearrange("p (a w) -> p a w", w=DIAG)
-        nc.vector.tensor_tensor(out=zb_cells[0:32, :, 0:L], in0=wb[0:32, :, 0:L], in1=mb[0:32, :, 0:L], op=MULT)
-        nc.vector.tensor_tensor(out=za_cells[:, 12:13, 0:L], in0=wa[:, 12:13, 0:L], in1=ma[:, 12:13, 0:L], op=MULT)
         spill0 = FRONT + 12 * S + 512
-        nc.vector.tensor_tensor(out=za[96:128, spill0 : spill0 + 64], in0=wp[96:128, :], in1=mp[96:128, :], op=MULT)
-        for a0 in (0, 4, 8):
-            nc.vector.tensor_tensor(
-                out=za_cells[:, a0 : a0 + 4, 0:L], in0=wa[:, a0 : a0 + 4, 0:L], in1=ma[:, a0 : a0 + 4, 0:L], op=MULT
-            )
-
         zaf = za[:].bitcast(F32)
         zbf = zb[:].bitcast(F32)
         gf = g[:].bitcast(F32).rearrange("p (q c n u) -> p q c n u", q=4, c=4, u=2)
         gsf = gs[:].bitcast(F32).rearrange("p (c n u) -> p c n u", c=4, u=2)
+        xf = x_sb[:].bitcast(F32)
+
+        def copy_out(engine, dst, src):
+            if engine == "s":
+                nc.scalar.copy(out=dst, in_=src)
+            else:
+                nc.vector.tensor_copy(out=dst, in_=src)
 
         def strip(pt, slot, zf, a):
             for uh in range(2):
@@ -147,56 +149,25 @@ def tile_structuredconnection_kernel(tc, x, weight, bias, mask, out):
                 in_=g[:, 2048 * q : 2048 * q + 2048],
             )
 
-        for a0 in range(0, 12, 2):
-            pt = tp.tile([P, 4, P], F32, tag="pt")
-            for slot in range(2):
-                a = a0 + slot
-                strip(pt, slot, zbf, a)
-                nc.scalar.copy(
-                    out=gf[:, 3, :, 32 + 8 * a : 40 + 8 * a, :],
-                    in_=pt[:, 2 * slot : 2 * slot + 2, 0:32].rearrange("p u (c n) -> p c n u", c=4),
-                )
-        pt = tp.tile([P, 4, P], F32, tag="pt")
-        strip(pt, 0, zaf, 12)
-        w0 = spill0 // 2
-        nc.tensor.transpose(pt[:, 2, :], zaf[:, w0 : w0 + P], ident[:])
-        nc.scalar.copy(out=gf[:, 3, :, 0:32, :], in_=pt[:, 0:2, :].rearrange("p u (c n) -> p c n u", c=4))
-        nc.scalar.copy(out=gsf[:, :, 0:32, 0], in_=pt[:, 2, :].rearrange("p (c n) -> p c n", c=4))
-        quantise_w(3)
-        nc.vector.quantize_mx(out=wsq[:].bitcast(FP8X4), scales=wss[:], in_=gs[:])
-        for a0 in range(0, 12, 2):
-            pt = tp.tile([P, 4, P], F32, tag="pt")
-            for slot in range(2):
-                a = a0 + slot
-                strip(pt, slot, zaf, a)
-                dst = gf[:, a // 4, :, 32 * (a % 4) : 32 * (a % 4) + 32, :]
-                src = pt[:, 2 * slot : 2 * slot + 2, :].rearrange("p u (c n) -> p c n u", c=4)
-                if slot == 0:
-                    nc.scalar.copy(out=dst, in_=src)
-                else:
-                    nc.vector.tensor_copy(out=dst, in_=src)
-            if a0 % 4 == 2:
-                quantise_w(a0 // 4)
+        xg_of = {}
 
-        xf = x_sb[:].bitcast(F32)
-
-        def prepare_x(mt):
-            xg = xgp.tile([P, 2048], BF16, align_bytes=64, tag="xg")
+        def x_bank(mt, h, engine):
+            if h == 0:
+                xg = xgp.tile([P, 2048], BF16, align_bytes=64, tag="xg")
+                xg_of[mt] = xg
+            xg = xg_of[mt]
             xgf = xg[:].bitcast(F32).rearrange("p (c m u) -> p c m u", c=4, u=2)
-            for h in range(2):
-                pt = tp.tile([P, 4, P], F32, tag="pt")
-                for k in range(4):
-                    w0 = mt * 1024 + 512 * h + 128 * k
-                    nc.tensor.transpose(pt[:, k, :], xf[:, w0 : w0 + P], ident[:])
-                src = pt[:].rearrange("p (c u) m -> p c m u", c=2)
-                if h == 1 and mt < 2:
-                    nc.vector.tensor_copy(out=xgf[:, 2 * h : 2 * h + 2, :, :], in_=src)
-                else:
-                    nc.scalar.copy(out=xgf[:, 2 * h : 2 * h + 2, :, :], in_=src)
+            pt = psum.tile([P, 4, P], F32, tag="bank")
+            for k in range(4):
+                w0 = mt * 1024 + 512 * h + 128 * k
+                nc.tensor.transpose(pt[:, k, :], xf[:, w0 : w0 + P], ident[:])
+            return engine, xgf[:, 2 * h : 2 * h + 2, :, :], pt[:].rearrange("p (c u) m -> p c m u", c=2)
+
+        def quantise_x(mt):
             nc.vector.quantize_mx(
                 out=xq[:, 512 * mt : 512 * mt + 512].bitcast(FP8X4),
                 scales=xs[:, 512 * mt : 512 * mt + 512],
-                in_=xg[:],
+                in_=xg_of[mt][:],
             )
 
         def x_operand(mt, c):
@@ -207,61 +178,122 @@ def tile_structuredconnection_kernel(tc, x, weight, bias, mask, out):
             v = t[:, b0 : b0 + 2048].rearrange("p (j r) -> p j r", r=256)[:, :, 0 : 51 * nv]
             return v.rearrange("p j (v s) -> p j v s", s=51)[:, :, :, 0:na]
 
-        def multiply(mt):
-            by_scalar = mt in SCALAR_TILES
-            o_sb = outp.tile([P, O + 256], F32, tag="o_sb")
-            for c in range(4):
-                acc = accp.tile([P, 512], F32, tag="acc")
-                lhs, lhs_s = x_operand(mt, c)
-                for q in range(4):
-                    lo = 512 * q + 128 * c
-                    nc.tensor.matmul_mx(
-                        out=acc[:, 128 * q : 128 * q + 128],
-                        lhsT=lhs,
-                        lhsT_scale=lhs_s,
-                        rhs=wq[:, lo : lo + 128].bitcast(FP8X4),
-                        rhs_scale=ws[:, lo : lo + 128],
-                        start=True,
-                        stop=(q < 3),
-                    )
-                lhs, lhs_s = x_operand(mt, (c + 1) % 4)
+        def passes(mt, c):
+            acc = psum.tile([P, 512], F32, tag="bank")
+            lhs, lhs_s = x_operand(mt, c)
+            for q in range(4):
+                lo = 512 * q + 128 * c
                 nc.tensor.matmul_mx(
-                    out=acc[:, 384:512],
+                    out=acc[:, 128 * q : 128 * q + 128],
                     lhsT=lhs,
                     lhsT_scale=lhs_s,
-                    rhs=wsq[:, 128 * c : 128 * c + 128].bitcast(FP8X4),
-                    rhs_scale=wss[:, 128 * c : 128 * c + 128],
-                    start=False,
-                    stop=True,
+                    rhs=wq[:, lo : lo + 128].bitcast(FP8X4),
+                    rhs_scale=ws[:, lo : lo + 128],
+                    start=True,
+                    stop=(q < 3),
                 )
-                pa = acc[:, 0:416].rearrange("p (a v j) -> p j v a", v=4, j=8)
-                for vp0, vp1, b0 in ((0, 3 - c, 64 * c + 103), (3 - c, 4, 64 * c - 153 + 51 * (3 - c))):
-                    nv = vp1 - vp0
-                    if nv > 0 and by_scalar:
-                        nc.scalar.copy(out=runs(o_sb, b0, nv, 13), in_=pa[:, :, vp0:vp1, :])
-                    elif nv > 0:
-                        nc.vector.tensor_tensor(
-                            out=runs(o_sb, b0, nv, 13), in0=pa[:, :, vp0:vp1, :], in1=runs(bias_bc, b0, nv, 13), op=ADD
-                        )
-                pb = acc[:, 416:512].rearrange("p (a j) -> p j a", j=8)
-                b0 = 64 * c + 52
-                o_run = o_sb[:, b0 : b0 + 2048].rearrange("p (j r) -> p j r", r=256)[:, :, 0:12]
-                if by_scalar:
-                    nc.scalar.copy(out=o_run, in_=pb)
-                else:
+            lhs, lhs_s = x_operand(mt, (c + 1) % 4)
+            nc.tensor.matmul_mx(
+                out=acc[:, 384:512],
+                lhsT=lhs,
+                lhsT_scale=lhs_s,
+                rhs=wsq[:, 128 * c : 128 * c + 128].bitcast(FP8X4),
+                rhs_scale=wss[:, 128 * c : 128 * c + 128],
+                start=False,
+                stop=True,
+            )
+            return acc
+
+        def evict(acc, o_sb, c, by_scalar):
+            pa = acc[:, 0:416].rearrange("p (a v j) -> p j v a", v=4, j=8)
+            for vp0, vp1, b0 in ((0, 3 - c, 64 * c + 103), (3 - c, 4, 64 * c - 153 + 51 * (3 - c))):
+                nv = vp1 - vp0
+                if nv > 0 and by_scalar:
+                    nc.scalar.copy(out=runs(o_sb, b0, nv, 13), in_=pa[:, :, vp0:vp1, :])
+                elif nv > 0:
                     nc.vector.tensor_tensor(
-                        out=o_run,
-                        in0=pb,
-                        in1=bias_bc[:, b0 : b0 + 2048].rearrange("p (j r) -> p j r", r=256)[:, :, 0:12],
-                        op=ADD,
+                        out=runs(o_sb, b0, nv, 13), in0=pa[:, :, vp0:vp1, :], in1=runs(bias_bc, b0, nv, 13), op=ADD
                     )
+            pb = acc[:, 416:512].rearrange("p (a j) -> p j a", j=8)
+            b0 = 64 * c + 52
+            o_run = o_sb[:, b0 : b0 + 2048].rearrange("p (j r) -> p j r", r=256)[:, :, 0:12]
             if by_scalar:
-                nc.gpsimd.tensor_tensor(out=o_sb[:, 0:O], in0=o_sb[:, 0:O], in1=bias_bc[:, 0:O], op=ADD)
-            nc.sync.dma_start(out=out[mt * P : (mt + 1) * P, :], in_=o_sb[:, 0:O])
+                nc.scalar.copy(out=o_run, in_=pb)
+            else:
+                nc.vector.tensor_tensor(
+                    out=o_run,
+                    in0=pb,
+                    in1=bias_bc[:, b0 : b0 + 2048].rearrange("p (j r) -> p j r", r=256)[:, :, 0:12],
+                    op=ADD,
+                )
+
+        def prepare_x(mt):
+            for h in range(2):
+                copy_out(*x_bank(mt, h, "v" if (h == 1 and mt % 2 == 0) else "s"))
+            quantise_x(mt)
 
         prepare_x(0)
         prepare_x(1)
-        for mt in range(MT):
-            if mt + 2 < MT:
-                prepare_x(mt + 2)
-            multiply(mt)
+
+        nc.vector.tensor_tensor(out=zb_cells[0:32, :, 0:L], in0=wb[0:32, :, 0:L], in1=mb[0:32, :, 0:L], op=MULT)
+        for a0 in range(0, 12, 2):
+            pt = psum.tile([P, 4, P], F32, tag="bank")
+            for slot in range(2):
+                strip(pt, slot, zbf, a0 + slot)
+            for slot in range(2):
+                a = a0 + slot
+                nc.scalar.copy(
+                    out=gf[:, 3, :, 32 + 8 * a : 40 + 8 * a, :],
+                    in_=pt[:, 2 * slot : 2 * slot + 2, 0:32].rearrange("p u (c n) -> p c n u", c=4),
+                )
+        for mt in range(2, MT):
+            prepare_x(mt)
+
+        for n in range(4):
+            bps = psum.tile([P, 512], F32, tag="bank")
+            nc.tensor.matmul(bps[:], lhsT=ones[:], rhs=bz[:, 512 * n : 512 * n + 512], start=True, stop=True)
+            nc.scalar.copy(out=bias_bc[:, 512 * n : 512 * n + 512], in_=bps[:])
+
+        nc.vector.tensor_tensor(out=za_cells[:, 12:13, 0:L], in0=wa[:, 12:13, 0:L], in1=ma[:, 12:13, 0:L], op=MULT)
+        nc.vector.tensor_tensor(out=za[96:128, spill0 : spill0 + 64], in0=wp[96:128, :], in1=mp[96:128, :], op=MULT)
+        for a0 in (0, 4, 8):
+            nc.vector.tensor_tensor(
+                out=za_cells[:, a0 : a0 + 4, 0:L], in0=wa[:, a0 : a0 + 4, 0:L], in1=ma[:, a0 : a0 + 4, 0:L], op=MULT
+            )
+        pt = psum.tile([P, 4, P], F32, tag="bank")
+        strip(pt, 0, zaf, 12)
+        nc.tensor.transpose(pt[:, 2, :], zaf[:, spill0 // 2 : spill0 // 2 + P], ident[:])
+        nc.scalar.copy(out=gf[:, 3, :, 0:32, :], in_=pt[:, 0:2, :].rearrange("p u (c n) -> p c n u", c=4))
+        nc.scalar.copy(out=gsf[:, :, 0:32, 0], in_=pt[:, 2, :].rearrange("p (c n) -> p c n", c=4))
+        quantise_w(3)
+        nc.vector.quantize_mx(out=wsq[:].bitcast(FP8X4), scales=wss[:], in_=gs[:])
+        for a0 in range(0, 12, 2):
+            pt = psum.tile([P, 4, P], F32, tag="bank")
+            for slot in range(2):
+                strip(pt, slot, zaf, a0 + slot)
+            for slot in range(2):
+                a = a0 + slot
+                copy_out(
+                    "s" if a0 % 4 == 0 else "v",
+                    gf[:, a // 4, :, 32 * (a % 4) : 32 * (a % 4) + 32, :],
+                    pt[:, 2 * slot : 2 * slot + 2, :].rearrange("p u (c n) -> p c n u", c=4),
+                )
+            if a0 % 4 == 2:
+                quantise_w(a0 // 4)
+
+        for pair in range(MT // 2):
+            ta, tb = 2 * pair, 2 * pair + 1
+            o_a = outp.tile([P, O + 256], F32, tag="o_sb")
+            o_b = outp.tile([P, O + 256], F32, tag="o_sb")
+            for c in range(4):
+                acc_a = passes(ta, c)
+                acc_b = passes(tb, c)
+                evict(acc_a, o_a, c, False)
+                evict(acc_b, o_b, c, True)
+            nc.sync.dma_start(out=out[ta * P : (ta + 1) * P, :], in_=o_a[:, 0:O])
+            for half in range(2):
+                lo = 1024 * half
+                nc.gpsimd.tensor_tensor(
+                    out=o_b[:, lo : lo + 1024], in0=o_b[:, lo : lo + 1024], in1=bias_bc[:, lo : lo + 1024], op=ADD
+                )
+                nc.sync.dma_start(out=out[tb * P : (tb + 1) * P, lo : lo + 1024], in_=o_b[:, lo : lo + 1024])

@@ -20,7 +20,8 @@ BYTES = M * K * 2 + M * O * 4 + 2 * O * 64 * 2 + O * 2
 
 FRONT = 32
 S = 576
-L = 120
+L = 128
+LM = 120
 LP = 128
 DIAG = S + 40
 ROWSTEP = K + 40
@@ -235,7 +236,7 @@ def tile_structuredconnection_kernel(tc, x, weight, bias, mask, out):
         prepare_x(0)
         prepare_x(1)
 
-        nc.vector.tensor_tensor(out=zb_cells[0:32, :, 0:L], in0=wb[0:32, :, 0:L], in1=mb[0:32, :, 0:L], op=MULT)
+        nc.vector.tensor_tensor(out=zb_cells[0:32, :, 0:LM], in0=wb[0:32, :, 0:LM], in1=mb[0:32, :, 0:LM], op=MULT)
         for a0 in range(0, 12, 2):
             pt = psum.tile([P, 4, P], F32, tag="bank")
             for slot in range(2):
@@ -254,11 +255,11 @@ def tile_structuredconnection_kernel(tc, x, weight, bias, mask, out):
             nc.tensor.matmul(bps[:], lhsT=ones[:], rhs=bz[:, 512 * n : 512 * n + 512], start=True, stop=True)
             nc.scalar.copy(out=bias_bc[:, 512 * n : 512 * n + 512], in_=bps[:])
 
-        nc.vector.tensor_tensor(out=za_cells[:, 12:13, 0:L], in0=wa[:, 12:13, 0:L], in1=ma[:, 12:13, 0:L], op=MULT)
+        nc.vector.tensor_tensor(out=za_cells[:, 12:13, 0:LM], in0=wa[:, 12:13, 0:LM], in1=ma[:, 12:13, 0:LM], op=MULT)
         nc.vector.tensor_tensor(out=za[96:128, spill0 : spill0 + 64], in0=wp[96:128, :], in1=mp[96:128, :], op=MULT)
         for a0 in (0, 4, 8):
             nc.vector.tensor_tensor(
-                out=za_cells[:, a0 : a0 + 4, 0:L], in0=wa[:, a0 : a0 + 4, 0:L], in1=ma[:, a0 : a0 + 4, 0:L], op=MULT
+                out=za_cells[:, a0 : a0 + 4, 0:LM], in0=wa[:, a0 : a0 + 4, 0:LM], in1=ma[:, a0 : a0 + 4, 0:LM], op=MULT
             )
         pt = psum.tile([P, 4, P], F32, tag="bank")
         strip(pt, 0, zaf, 12)

@@ -18,14 +18,13 @@ MT = M // P
 FLOPS = 2 * M * O * 64
 BYTES = M * K * 2 + M * O * 4 + 2 * O * 64 * 2 + O * 2
 
+S = 704
 FRONT = 32
-S = 576
 L = 128
-LM = 120
-LP = 128
-DIAG = S + 40
+STRIPS = 24
+ZLIVE = FRONT + S * (STRIPS - 1) + 768
+ZW = FRONT + S * STRIPS + 640
 ROWSTEP = K + 40
-CELL0 = FRONT - 24
 
 
 def tile_structuredconnection_kernel(tc, x, weight, bias, mask, out):
@@ -33,24 +32,19 @@ def tile_structuredconnection_kernel(tc, x, weight, bias, mask, out):
     with ExitStack() as ctx:
         keep = ctx.enter_context(tc.tile_pool(name="keep", bufs=1))
         xgp = ctx.enter_context(tc.tile_pool(name="xgp", bufs=3))
-        outp = ctx.enter_context(tc.tile_pool(name="outp", bufs=4))
+        outp = ctx.enter_context(tc.tile_pool(name="outp", bufs=6))
         psum = ctx.enter_context(tc.psum_pool(name="psum", bufs=8))
         ctx.enter_context(tc.manual_schedule())
 
-        wa = keep.tile([P, 13, LP], BF16)
-        ma = keep.tile([P, 13, LP], BF16)
-        wb = keep.tile([P, 12, LP], BF16)
-        mb = keep.tile([P, 12, LP], BF16)
-        wp = keep.tile([P, 64], BF16)
-        mp = keep.tile([P, 64], BF16)
-        za = keep.tile([P, CELL0 + 13 * DIAG], BF16, align_bytes=64)
-        zb = keep.tile([P, CELL0 + 12 * DIAG], BF16, align_bytes=64)
+        wa = keep.tile([P, STRIPS, L], BF16)
+        ma = keep.tile([P, STRIPS, L], BF16)
+        z = keep.tile([P, ZW], BF16, align_bytes=64)
         g = keep.tile([P, 8192], BF16, align_bytes=64)
-        gs = keep.tile([P, 2048], BF16, align_bytes=64)
+        gs = keep.tile([P, 4096], BF16, align_bytes=64)
         wq = keep.tile([P, 2048], U32, align_bytes=64)
         ws = keep.tile([P, 2048], U8, align_bytes=64)
-        wsq = keep.tile([P, 512], U32, align_bytes=64)
-        wss = keep.tile([P, 512], U8, align_bytes=64)
+        wsq = keep.tile([P, 1024], U32, align_bytes=64)
+        wss = keep.tile([P, 1024], U8, align_bytes=64)
         x_sb = keep.tile([P, MT * K], BF16, align_bytes=64)
         xq = keep.tile([P, MT * 512], U32, align_bytes=64)
         xs = keep.tile([P, MT * 512], U8, align_bytes=64)
@@ -61,26 +55,20 @@ def tile_structuredconnection_kernel(tc, x, weight, bias, mask, out):
 
         nc.vector.memset(wa[0:32, 0, 0:32], 0.0)
         nc.vector.memset(ma[0:32, 0, 0:32], 0.0)
-        nc.vector.memset(wb[0:32, 11, 96:LP], 0.0)
-        nc.vector.memset(mb[0:32, 11, 96:LP], 0.0)
+        nc.vector.memset(wa[32:64, 11, 64:L], 0.0)
+        nc.vector.memset(ma[32:64, 11, 64:L], 0.0)
         make_identity(nc, ident[:])
 
         wj = weight.rearrange("(j r) k -> j (r k)", j=8)
         mj = mask.rearrange("(j r) k -> j (r k)", j=8)
 
-        def cells(src, base, c, a0, a1, i0, i1):
-            s0 = (base + a0) * K + 512 * c + 40 * a0 - 24
-            n = a1 - a0
+        def load(src, dst, p0, d0, row, col, n, i0, i1):
+            s0 = row * K + col
             if n == 1:
-                return src[:, s0 + i0 : s0 + i1]
-            assert s0 >= 0 and s0 + n * ROWSTEP <= 256 * K
-            return src[:, s0 : s0 + n * ROWSTEP].rearrange("j (a w) -> j a w", w=ROWSTEP)[:, :, i0:i1]
-
-        def load(queue, src, dst, p0, base, c, a0, a1, i0, i1):
-            if a1 - a0 == 1:
-                queue.dma_start(out=dst[p0 : p0 + 8, a0, i0:i1], in_=cells(src, base, c, a0, a1, i0, i1))
+                nc.sync.dma_start(out=dst[p0 : p0 + 8, d0, i0:i1], in_=src[:, s0 + i0 : s0 + i1])
             else:
-                queue.dma_start(out=dst[p0 : p0 + 8, a0:a1, i0:i1], in_=cells(src, base, c, a0, a1, i0, i1))
+                rows = src[:, s0 : s0 + n * ROWSTEP].rearrange("j (a w) -> j a w", w=ROWSTEP)
+                nc.sync.dma_start(out=dst[p0 : p0 + 8, d0 : d0 + n, i0:i1], in_=rows[:, :, i0:i1])
 
         def load_x(t0):
             nc.sync.dma_start(
@@ -88,47 +76,42 @@ def tile_structuredconnection_kernel(tc, x, weight, bias, mask, out):
                 in_=x[t0 * P : (t0 + 2) * P, :].rearrange("(t p) k -> p t k", p=P),
             )
 
-        both = ((wj, wa, wb, wp), (mj, ma, mb, mp))
-        load_x(0)
-        for src, dst_a, dst_b, dst_p in both:
+        def load_h(h):
             for c in range(4):
-                base = 64 * c + 52
-                if c == 3:
-                    load(nc.sync, src, dst_b, 8 * c, base, c, 0, 11, 0, L)
-                    load(nc.sync, src, dst_b, 8 * c, base, c, 11, 12, 0, 96)
-                else:
-                    load(nc.sync, src, dst_b, 8 * c, base, c, 0, 12, 0, L)
+                row = (64 * c + 52 * h) % 256
+                col = 512 * c + 32 * h - 24
+                p0 = 32 * (h % 4) + 8 * c if h < 4 else 32 + 8 * c
+                d0 = 0 if h < 4 else 12
+                for src, dst in ((wj, wa), (mj, ma)):
+                    if h == 0 and c == 0:
+                        load(src, dst, p0, 1, row + 1, col + 40, 15, 0, L)
+                        load(src, dst, p0, 0, row, col, 1, 24, L)
+                    elif h == 1 and c == 3:
+                        load(src, dst, p0, 0, row, col, 11, 0, L)
+                        load(src, dst, p0, 11, row + 11, col + 440, 1, 0, 64)
+                    else:
+                        load(src, dst, p0, d0, row, col, 16 if h == 0 else 12, 0, L)
+
+        load_x(0)
+        load_h(0)
+        load_h(4)
+        load_h(1)
+        load_h(2)
+        load_h(3)
         load_x(2)
         load_x(4)
         load_x(6)
-        for src, dst_a, dst_b, dst_p in both:
-            for c in range(4):
-                for vp in range(4):
-                    v = 3 - vp
-                    base = 64 * ((c - v) % 4) + 13 * v
-                    p0 = 8 * (4 * c + vp)
-                    if c == 0 and v == 0:
-                        load(nc.sync, src, dst_a, p0, base, c, 1, 13, 0, L)
-                        load(nc.sync, src, dst_a, p0, base, c, 0, 1, 24, L)
-                    else:
-                        load(nc.sync, src, dst_a, p0, base, c, 0, 13, 0, L)
-                    if c == 3:
-                        r0 = (base + 12) * K
-                        nc.sync.dma_start(out=dst_p[p0 : p0 + 8, :], in_=src[:, r0 : r0 + 64])
         nc.gpsimd.memset(bz[:].bitcast(F32), 0.0)
         nc.scalar.dma_start(out=bz[0:1, :], in_=bias.rearrange("(o n) -> o n", o=1))
 
+        zhalf = FRONT + 12 * S
+        nc.vector.memset(z[:, 0:zhalf].bitcast(I32), 0)
         nc.gpsimd.memset(ones[:], 1.0)
-        nc.vector.memset(za[:].bitcast(I32)[:, 0 : (FRONT + 12 * S + 768) // 2], 0)
-        nc.gpsimd.memset(zb[:].bitcast(F32)[:, 0 : (CELL0 + 11 * DIAG + L) // 2], 0.0)
-        nc.vector.memset(gs[:].bitcast(I32), 0)
+        nc.gpsimd.memset(z[:, zhalf:ZLIVE].bitcast(F32), 0.0)
+        nc.gpsimd.memset(gs[:].bitcast(F32), 0.0)
 
-        za_cells = za[:, CELL0 : CELL0 + 13 * DIAG].rearrange("p (a w) -> p a w", w=DIAG)
-        zb_cells = zb[:, CELL0 : CELL0 + 12 * DIAG].rearrange("p (a w) -> p a w", w=DIAG)
-        spill0 = FRONT + 12 * S + 512
-        zaf = za[:].bitcast(F32)
-        zbf = zb[:].bitcast(F32)
-        gf = g[:].bitcast(F32).rearrange("p (q c n u) -> p q c n u", q=4, c=4, u=2)
+        zf = z[:].bitcast(F32)
+        gf = g[:].bitcast(F32).rearrange("p (c n u) -> p c n u", c=4, u=2)
         gsf = gs[:].bitcast(F32).rearrange("p (c n u) -> p c n u", c=4, u=2)
         xf = x_sb[:].bitcast(F32)
 
@@ -138,16 +121,38 @@ def tile_structuredconnection_kernel(tc, x, weight, bias, mask, out):
             else:
                 nc.vector.tensor_copy(out=dst, in_=src)
 
-        def strip(pt, slot, zf, a):
+        def strip(pt, slot, i):
             for uh in range(2):
-                w0 = (FRONT + S * a + 256 * uh) // 2
+                w0 = (FRONT + S * i + 256 * uh) // 2
                 nc.tensor.transpose(pt[:, 2 * slot + uh, :], zf[:, w0 : w0 + P], ident[:])
 
-        def quantise_w(q):
+        def spill(pt, slot, i):
+            w0 = (FRONT + S * i + 512) // 2
+            nc.tensor.transpose(pt[:, slot, :], zf[:, w0 : w0 + P], ident[:])
+
+        def multiply(q, i0, n, off):
+            p0 = 32 * q
+            s0 = FRONT + S * i0 + off - 24
+            dst = z[p0 : p0 + 32, s0 : s0 + n * (S + 40)].rearrange("p (a w) -> p a w", w=S + 40)
+            nc.vector.tensor_tensor(
+                out=dst[:, :, 0:L],
+                in0=wa[p0 : p0 + 32, i0 : i0 + n, :],
+                in1=ma[p0 : p0 + 32, i0 : i0 + n, :],
+                op=MULT,
+            )
+
+        def quantise_w(c):
             nc.vector.quantize_mx(
-                out=wq[:, 512 * q : 512 * q + 512].bitcast(FP8X4),
-                scales=ws[:, 512 * q : 512 * q + 512],
-                in_=g[:, 2048 * q : 2048 * q + 2048],
+                out=wq[:, 512 * c : 512 * c + 512].bitcast(FP8X4),
+                scales=ws[:, 512 * c : 512 * c + 512],
+                in_=g[:, 2048 * c : 2048 * c + 2048],
+            )
+
+        def quantise_spill(half):
+            nc.vector.quantize_mx(
+                out=wsq[:, 512 * half : 512 * half + 512].bitcast(FP8X4),
+                scales=wss[:, 512 * half : 512 * half + 512],
+                in_=gs[:, 2048 * half : 2048 * half + 2048],
             )
 
         xg_of = {}
@@ -162,7 +167,7 @@ def tile_structuredconnection_kernel(tc, x, weight, bias, mask, out):
             for k in range(4):
                 w0 = mt * 1024 + 512 * h + 128 * k
                 nc.tensor.transpose(pt[:, k, :], xf[:, w0 : w0 + P], ident[:])
-            return engine, xgf[:, 2 * h : 2 * h + 2, :, :], pt[:].rearrange("p (c u) m -> p c m u", c=2)
+            copy_out(engine, xgf[:, 2 * h : 2 * h + 2, :, :], pt[:].rearrange("p (c u) m -> p c m u", c=2))
 
         def quantise_x(mt):
             nc.vector.quantize_mx(
@@ -175,126 +180,153 @@ def tile_structuredconnection_kernel(tc, x, weight, bias, mask, out):
             lo = 512 * mt + 128 * c
             return xq[:, lo : lo + 128].bitcast(FP8X4), xs[:, lo : lo + 128]
 
-        def runs(t, b0, nv, na):
-            v = t[:, b0 : b0 + 2048].rearrange("p (j r) -> p j r", r=256)[:, :, 0 : 51 * nv]
-            return v.rearrange("p j (v s) -> p j v s", s=51)[:, :, :, 0:na]
-
         def passes(mt, c):
             acc = psum.tile([P, 512], F32, tag="bank")
             lhs, lhs_s = x_operand(mt, c)
-            for q in range(4):
-                lo = 512 * q + 128 * c
+            for n0 in (0, 256):
+                lo = 512 * c + n0
                 nc.tensor.matmul_mx(
-                    out=acc[:, 128 * q : 128 * q + 128],
+                    out=acc[:, n0 : n0 + 256],
                     lhsT=lhs,
                     lhsT_scale=lhs_s,
-                    rhs=wq[:, lo : lo + 128].bitcast(FP8X4),
-                    rhs_scale=ws[:, lo : lo + 128],
+                    rhs=wq[:, lo : lo + 256].bitcast(FP8X4),
+                    rhs_scale=ws[:, lo : lo + 256],
                     start=True,
-                    stop=(q < 3),
+                    stop=(n0 == 0),
                 )
             lhs, lhs_s = x_operand(mt, (c + 1) % 4)
             nc.tensor.matmul_mx(
-                out=acc[:, 384:512],
+                out=acc[:, 256:512],
                 lhsT=lhs,
                 lhsT_scale=lhs_s,
-                rhs=wsq[:, 128 * c : 128 * c + 128].bitcast(FP8X4),
-                rhs_scale=wss[:, 128 * c : 128 * c + 128],
+                rhs=wsq[:, 256 * c : 256 * c + 256].bitcast(FP8X4),
+                rhs_scale=wss[:, 256 * c : 256 * c + 256],
                 start=False,
                 stop=True,
             )
             return acc
 
-        def evict(acc, o_sb, c, by_scalar):
-            pa = acc[:, 0:416].rearrange("p (a v j) -> p j v a", v=4, j=8)
-            for vp0, vp1, b0 in ((0, 3 - c, 64 * c + 103), (3 - c, 4, 64 * c - 153 + 51 * (3 - c))):
-                nv = vp1 - vp0
-                if nv > 0 and by_scalar:
-                    nc.scalar.copy(out=runs(o_sb, b0, nv, 13), in_=pa[:, :, vp0:vp1, :])
-                elif nv > 0:
-                    nc.vector.tensor_tensor(
-                        out=runs(o_sb, b0, nv, 13), in0=pa[:, :, vp0:vp1, :], in1=runs(bias_bc, b0, nv, 13), op=ADD
-                    )
-            pb = acc[:, 416:512].rearrange("p (a j) -> p j a", j=8)
-            b0 = 64 * c + 52
-            o_run = o_sb[:, b0 : b0 + 2048].rearrange("p (j r) -> p j r", r=256)[:, :, 0:12]
+        def out_runs(t, b0, nh):
+            v = t[:, b0 : b0 + 2048].rearrange("p (j r) -> p j r", r=256)[:, :, 0 : 52 * nh]
+            return v.rearrange("p j (h e) -> p j h e", e=52)[:, :, :, 0:12]
+
+        def leave(by_scalar, dst, src, b):
             if by_scalar:
-                nc.scalar.copy(out=o_run, in_=pb)
+                nc.scalar.copy(out=dst, in_=src)
             else:
-                nc.vector.tensor_tensor(
-                    out=o_run,
-                    in0=pb,
-                    in1=bias_bc[:, b0 : b0 + 2048].rearrange("p (j r) -> p j r", r=256)[:, :, 0:12],
-                    op=ADD,
-                )
+                nc.vector.tensor_tensor(out=dst, in0=src, in1=b, op=ADD)
 
-        def prepare_x(mt):
+        def evict(acc, o_sb, c, by_scalar):
+            pa = acc[:, 0:480].rearrange("p (h a j) -> p j h a", h=5, a=12)
+            split = (4, 4, 3, 2)[c]
+            for h0, h1 in ((0, split), (split, 5)):
+                b0 = (64 * c + 52 * h0) % 256
+                leave(by_scalar, out_runs(o_sb, b0, h1 - h0), pa[:, :, h0:h1, :], out_runs(bias_bc, b0, h1 - h0))
+            pb = acc[:, 480:512].rearrange("p (s j) -> p j s", s=4)
+            b0 = 64 * c + 12
+            o_run = o_sb[:, b0 : b0 + 2048].rearrange("p (j r) -> p j r", r=256)[:, :, 0:4]
+            b_run = bias_bc[:, b0 : b0 + 2048].rearrange("p (j r) -> p j r", r=256)[:, :, 0:4]
+            leave(by_scalar, o_run, pb, b_run)
+
+        for mt in range(2):
             for h in range(2):
-                copy_out(*x_bank(mt, h, "v" if (h == 1 and mt % 2 == 0) else "s"))
+                x_bank(mt, h, "v" if h == 1 else "s")
             quantise_x(mt)
-
-        prepare_x(0)
-        prepare_x(1)
-
-        nc.vector.tensor_tensor(out=zb_cells[0:32, :, 0:LM], in0=wb[0:32, :, 0:LM], in1=mb[0:32, :, 0:LM], op=MULT)
-        for a0 in range(0, 12, 2):
-            pt = psum.tile([P, 4, P], F32, tag="bank")
-            for slot in range(2):
-                strip(pt, slot, zbf, a0 + slot)
-            for slot in range(2):
-                a = a0 + slot
-                nc.scalar.copy(
-                    out=gf[:, 3, :, 32 + 8 * a : 40 + 8 * a, :],
-                    in_=pt[:, 2 * slot : 2 * slot + 2, 0:32].rearrange("p u (c n) -> p c n u", c=4),
-                )
-        for mt in range(2, MT):
-            prepare_x(mt)
 
         for n in range(4):
             bps = psum.tile([P, 512], F32, tag="bank")
             nc.tensor.matmul(bps[:], lhsT=ones[:], rhs=bz[:, 512 * n : 512 * n + 512], start=True, stop=True)
             nc.scalar.copy(out=bias_bc[:, 512 * n : 512 * n + 512], in_=bps[:])
 
-        nc.vector.tensor_tensor(out=za_cells[:, 12:13, 0:LM], in0=wa[:, 12:13, 0:LM], in1=ma[:, 12:13, 0:LM], op=MULT)
-        nc.vector.tensor_tensor(out=za[96:128, spill0 : spill0 + 64], in0=wp[96:128, :], in1=mp[96:128, :], op=MULT)
-        for a0 in (0, 4, 8):
-            nc.vector.tensor_tensor(
-                out=za_cells[:, a0 : a0 + 4, 0:LM], in0=wa[:, a0 : a0 + 4, 0:LM], in1=ma[:, a0 : a0 + 4, 0:LM], op=MULT
-            )
-        pt = psum.tile([P, 4, P], F32, tag="bank")
-        strip(pt, 0, zaf, 12)
-        nc.tensor.transpose(pt[:, 2, :], zaf[:, spill0 // 2 : spill0 // 2 + P], ident[:])
-        nc.scalar.copy(out=gf[:, 3, :, 0:32, :], in_=pt[:, 0:2, :].rearrange("p u (c n) -> p c n u", c=4))
-        nc.scalar.copy(out=gsf[:, :, 0:32, 0], in_=pt[:, 2, :].rearrange("p (c n) -> p c n", c=4))
-        quantise_w(3)
-        nc.vector.quantize_mx(out=wsq[:].bitcast(FP8X4), scales=wss[:], in_=gs[:])
-        for a0 in range(0, 12, 2):
+        def gs_cols(c0, c1, n0, n):
+            return gsf[0:64, c0:c1, n0 : n0 + 8 * n, 0].rearrange("p c (s j) -> p c s j", s=n)
+
+        def spill_cols(pt, s0, n, q, c0, c1):
+            lo = 32 * q + 8 * c0
+            src = pt[0:64, s0 : s0 + n, lo : lo + 8 * (c1 - c0)]
+            return src.rearrange("p s (c j) -> p c s j", c=c1 - c0)
+
+        def spill_copy(pt, n0, n, q, slot):
+            nc.scalar.copy(out=gs_cols(0, 3, n0, n), in_=spill_cols(pt, slot, n, q, 0, 3))
+            nc.scalar.copy(out=gs_cols(3, 4, n0, n), in_=spill_cols(pt, slot - 1, n, q, 3, 4))
+
+        multiply(0, 0, 16, 0)
+        multiply(1, 12, 12, 128)
+        for s0 in (0, 2):
             pt = psum.tile([P, 4, P], F32, tag="bank")
             for slot in range(2):
-                strip(pt, slot, zaf, a0 + slot)
+                strip(pt, slot, 12 + s0 + slot)
+            ptv = pt[:].rearrange("p (s u) (q c j) -> p q c s j u", s=2, q=4, c=4)
+            for q, n0 in ((0, 480), (1, 384)):
+                dst = gf[:, :, n0 + 8 * s0 : n0 + 8 * s0 + 16, :].rearrange("p c (s j) u -> p c s j u", s=2)
+                nc.scalar.copy(out=dst, in_=ptv[:, q])
+        for i in range(16, 24, 2):
+            pt = psum.tile([P, 4, P], F32, tag="bank")
             for slot in range(2):
-                a = a0 + slot
+                strip(pt, slot, i + slot)
+            ptv = pt[:].rearrange("p (s u) (q c j) -> p q c s j u", s=2, q=4, c=4)
+            n0 = 384 + 8 * (i - 12)
+            dst = gf[:, :, n0 : n0 + 16, :].rearrange("p c (s j) u -> p c s j u", s=2)
+            copy_out("v" if i % 4 == 0 else "s", dst, ptv[:, 1])
+        pt = psum.tile([P, 4, P], F32, tag="bank")
+        for slot in range(4):
+            spill(pt, slot, 12 + slot)
+        nc.scalar.copy(out=gs_cols(0, 3, 224, 4), in_=spill_cols(pt, 0, 4, 0, 0, 3))
+        nc.scalar.copy(out=gs_cols(3, 4, 232, 3), in_=spill_cols(pt, 0, 3, 0, 3, 4))
+        pt = psum.tile([P, 4, P], F32, tag="bank")
+        for slot in range(4):
+            spill(pt, slot, 20 + slot)
+        spill_copy(pt, 200, 3, 1, 1)
+        multiply(1, 0, 12, 32)
+        multiply(2, 0, 12, 64)
+        multiply(3, 0, 12, 96)
+        pt = psum.tile([P, 4, P], F32, tag="bank")
+        for slot in range(3):
+            spill(pt, slot, 9 + slot)
+        spill_copy(pt, 24, 1, 2, 2)
+        spill_copy(pt, 112, 2, 3, 1)
+        nc.scalar.copy(out=gs_cols(3, 4, 224, 1), in_=spill_cols(pt, 2, 1, 0, 3, 4))
+        for i in range(0, 12, 2):
+            pt = psum.tile([P, 4, P], F32, tag="bank")
+            for slot in range(2):
+                strip(pt, slot, i + slot)
+            for slot in range(2):
+                dst = gf[:, :, 0:384, :].rearrange("p c (h a j) u -> p h c a j u", h=4, a=12)
                 copy_out(
-                    "s" if a0 % 4 == 0 else "v",
-                    gf[:, a // 4, :, 32 * (a % 4) : 32 * (a % 4) + 32, :],
-                    pt[:, 2 * slot : 2 * slot + 2, :].rearrange("p u (c n) -> p c n u", c=4),
+                    "s" if i % 4 == 0 else "v",
+                    dst[:, :, :, i + slot],
+                    pt[:, 2 * slot : 2 * slot + 2, :].rearrange("p u (h c j) -> p h c j u", h=4, c=4),
                 )
-            if a0 % 4 == 2:
-                quantise_w(a0 // 4)
+        quantise_w(0)
+        quantise_spill(0)
+        quantise_w(1)
 
         for pair in range(MT // 2):
             ta, tb = 2 * pair, 2 * pair + 1
             o_a = outp.tile([P, O + 256], F32, tag="o_sb")
             o_b = outp.tile([P, O + 256], F32, tag="o_sb")
+            last = pair == MT // 2 - 1
             for c in range(4):
-                acc_a = passes(ta, c)
                 acc_b = passes(tb, c)
-                evict(acc_a, o_a, c, False)
-                evict(acc_b, o_b, c, True)
-            nc.sync.dma_start(out=out[ta * P : (ta + 1) * P, :], in_=o_a[:, 0:O])
+                acc_a = passes(ta, c)
+                if c == 3 and not last:
+                    quantise_x(ta + 2)
+                evict(acc_b, o_b, c, False)
+                evict(acc_a, o_a, c, not last)
+                if pair == 0 and c == 0:
+                    quantise_spill(1)
+                    quantise_w(2)
+                if pair == 0 and c == 1:
+                    quantise_w(3)
+                if c < 2 and not last:
+                    for h in range(2):
+                        x_bank(ta + 2 + c, h, "s")
+            if not last:
+                quantise_x(tb + 2)
+            nc.sync.dma_start(out=out[tb * P : (tb + 1) * P, :], in_=o_b[:, 0:O])
             for half in range(2):
                 lo = 1024 * half
-                nc.gpsimd.tensor_tensor(
-                    out=o_b[:, lo : lo + 1024], in0=o_b[:, lo : lo + 1024], in1=bias_bc[:, lo : lo + 1024], op=ADD
-                )
-                nc.sync.dma_start(out=out[tb * P : (tb + 1) * P, lo : lo + 1024], in_=o_b[:, lo : lo + 1024])
+                o_half = o_a[:, lo : lo + 1024]
+                if not last:
+                    nc.gpsimd.tensor_tensor(out=o_half, in0=o_half, in1=bias_bc[:, lo : lo + 1024], op=ADD)
+                nc.sync.dma_start(out=out[ta * P : (ta + 1) * P, lo : lo + 1024], in_=o_half)

@@ -15,6 +15,7 @@ MULT = mybir.AluOpType.mult
 P = 128
 M, K, O = 1024, 2048, 2048
 MT = M // P
+S_TILES = (0, 2, 4)
 FLOPS = 2 * M * O * 64
 BYTES = M * K * 2 + M * O * 4 + 2 * O * 64 * 2 + O * 2
 
@@ -40,11 +41,11 @@ def tile_structuredconnection_kernel(tc, x, weight, bias, mask, out):
         ma = keep.tile([P, STRIPS, L], BF16)
         z = keep.tile([P, ZW], BF16, align_bytes=64)
         g = keep.tile([P, 8192], BF16, align_bytes=64)
-        gs = keep.tile([P, 4096], BF16, align_bytes=64)
+        gs = keep.tile([P, 2048], BF16, align_bytes=64)
         wq = keep.tile([P, 2048], U32, align_bytes=64)
         ws = keep.tile([P, 2048], U8, align_bytes=64)
-        wsq = keep.tile([P, 1024], U32, align_bytes=64)
-        wss = keep.tile([P, 1024], U8, align_bytes=64)
+        wsq = keep.tile([P, 512], U32, align_bytes=64)
+        wss = keep.tile([P, 512], U8, align_bytes=64)
         x_sb = keep.tile([P, MT * K], BF16, align_bytes=64)
         xq = keep.tile([P, MT * 512], U32, align_bytes=64)
         xs = keep.tile([P, MT * 512], U8, align_bytes=64)
@@ -148,12 +149,8 @@ def tile_structuredconnection_kernel(tc, x, weight, bias, mask, out):
                 in_=g[:, 2048 * c : 2048 * c + 2048],
             )
 
-        def quantise_spill(half):
-            nc.vector.quantize_mx(
-                out=wsq[:, 512 * half : 512 * half + 512].bitcast(FP8X4),
-                scales=wss[:, 512 * half : 512 * half + 512],
-                in_=gs[:, 2048 * half : 2048 * half + 2048],
-            )
+        def quantise_spill():
+            nc.vector.quantize_mx(out=wsq[:].bitcast(FP8X4), scales=wss[:], in_=gs[:])
 
         xg_of = {}
 
@@ -183,50 +180,56 @@ def tile_structuredconnection_kernel(tc, x, weight, bias, mask, out):
         def passes(mt, c):
             acc = psum.tile([P, 512], F32, tag="bank")
             lhs, lhs_s = x_operand(mt, c)
-            for n0 in (0, 256):
-                lo = 512 * c + n0
+            for n0, n1 in ((0, 256), (256, 384), (384, 512)):
+                lo, hi = 512 * c + n0, 512 * c + n1
                 nc.tensor.matmul_mx(
-                    out=acc[:, n0 : n0 + 256],
+                    out=acc[:, n0:n1],
                     lhsT=lhs,
                     lhsT_scale=lhs_s,
-                    rhs=wq[:, lo : lo + 256].bitcast(FP8X4),
-                    rhs_scale=ws[:, lo : lo + 256],
+                    rhs=wq[:, lo:hi].bitcast(FP8X4),
+                    rhs_scale=ws[:, lo:hi],
                     start=True,
-                    stop=(n0 == 0),
+                    stop=(n1 < 512),
                 )
             lhs, lhs_s = x_operand(mt, (c + 1) % 4)
             nc.tensor.matmul_mx(
-                out=acc[:, 256:512],
+                out=acc[:, 384:512],
                 lhsT=lhs,
                 lhsT_scale=lhs_s,
-                rhs=wsq[:, 256 * c : 256 * c + 256].bitcast(FP8X4),
-                rhs_scale=wss[:, 256 * c : 256 * c + 256],
+                rhs=wsq[:, 128 * c : 128 * c + 128].bitcast(FP8X4),
+                rhs_scale=wss[:, 128 * c : 128 * c + 128],
                 start=False,
                 stop=True,
             )
             return acc
 
-        def out_runs(t, b0, nh):
-            v = t[:, b0 : b0 + 2048].rearrange("p (j r) -> p j r", r=256)[:, :, 0 : 52 * nh]
-            return v.rearrange("p j (h e) -> p j h e", e=52)[:, :, :, 0:12]
+        def out_runs(t, c, h0, nh, a0, na):
+            b0 = (64 * c + 52 * h0) % 256
+            v = t[:, b0 : b0 + 2048].rearrange("p (j r) -> p j r", r=256)
+            if nh == 1:
+                return v[:, :, a0 : a0 + na]
+            return v[:, :, 0 : 52 * nh].rearrange("p j (h e) -> p j h e", e=52)[:, :, :, a0 : a0 + na]
 
-        def leave(by_scalar, dst, src, b):
-            if by_scalar:
-                nc.scalar.copy(out=dst, in_=src)
-            else:
-                nc.vector.tensor_tensor(out=dst, in0=src, in1=b, op=ADD)
+        def sum_cols(acc, n0, nh, na):
+            v = acc[:, n0 : n0 + 8 * nh * na]
+            if nh == 1:
+                return v.rearrange("p (j a) -> p j a", j=8)
+            return v.rearrange("p (h j a) -> p j h a", h=nh, j=8)
 
         def evict(acc, o_sb, c, by_scalar):
-            pa = acc[:, 0:480].rearrange("p (h a j) -> p j h a", h=5, a=12)
-            split = (4, 4, 3, 2)[c]
-            for h0, h1 in ((0, split), (split, 5)):
-                b0 = (64 * c + 52 * h0) % 256
-                leave(by_scalar, out_runs(o_sb, b0, h1 - h0), pa[:, :, h0:h1, :], out_runs(bias_bc, b0, h1 - h0))
-            pb = acc[:, 480:512].rearrange("p (s j) -> p j s", s=4)
-            b0 = 64 * c + 12
-            o_run = o_sb[:, b0 : b0 + 2048].rearrange("p (j r) -> p j r", r=256)[:, :, 0:4]
-            b_run = bias_bc[:, b0 : b0 + 2048].rearrange("p (j r) -> p j r", r=256)[:, :, 0:4]
-            leave(by_scalar, o_run, pb, b_run)
+            wrap = (5, 4, 3, 2)[c]
+            parts = [(0, 0, 2, 0, 12)]
+            for h0, h1 in ((2, wrap), (wrap, 5)):
+                if h0 < h1:
+                    parts.append((192 + 64 * (h0 - 2), h0, h1 - h0, 0, 8))
+                    parts.append((384 + 32 * (h0 - 2), h0, h1 - h0, 8, 4))
+            parts.append((480, 0, 1, 12, 4))
+            for n0, h0, nh, a0, na in parts:
+                dst, src = out_runs(o_sb, c, h0, nh, a0, na), sum_cols(acc, n0, nh, na)
+                if by_scalar:
+                    nc.scalar.copy(out=dst, in_=src)
+                else:
+                    nc.vector.tensor_tensor(out=dst, in0=src, in1=out_runs(bias_bc, c, h0, nh, a0, na), op=ADD)
 
         for mt in range(2):
             for h in range(2):
@@ -238,95 +241,105 @@ def tile_structuredconnection_kernel(tc, x, weight, bias, mask, out):
             nc.tensor.matmul(bps[:], lhsT=ones[:], rhs=bz[:, 512 * n : 512 * n + 512], start=True, stop=True)
             nc.scalar.copy(out=bias_bc[:, 512 * n : 512 * n + 512], in_=bps[:])
 
-        def gs_cols(c0, c1, n0, n):
-            return gsf[0:64, c0:c1, n0 : n0 + 8 * n, 0].rearrange("p c (s j) -> p c s j", s=n)
+        def g_cols(n0, pitch, a):
+            v = gf[:, :, n0 : n0 + 8 * pitch, :].rearrange("p c (j a) u -> p c j a u", j=8)
+            return v[:, :, :, a : a + 2, :]
 
-        def spill_cols(pt, s0, n, q, c0, c1):
+        def gs_cols(c0, c1, n0, s0, n):
+            v = gsf[0:64, c0:c1, n0 : n0 + 32, 0].rearrange("p c (j s) -> p c j s", s=4)
+            return v[:, :, :, s0 : s0 + n]
+
+        def spill_cols(pt, slot, n, q, c0, c1):
             lo = 32 * q + 8 * c0
-            src = pt[0:64, s0 : s0 + n, lo : lo + 8 * (c1 - c0)]
-            return src.rearrange("p s (c j) -> p c s j", c=c1 - c0)
+            src = pt[0:64, slot : slot + n, lo : lo + 8 * (c1 - c0)]
+            return src.rearrange("p s (c j) -> p c j s", c=c1 - c0)
 
-        def spill_copy(pt, n0, n, q, slot):
-            nc.scalar.copy(out=gs_cols(0, 3, n0, n), in_=spill_cols(pt, slot, n, q, 0, 3))
-            nc.scalar.copy(out=gs_cols(3, 4, n0, n), in_=spill_cols(pt, slot - 1, n, q, 3, 4))
+        def spill_copy(pt, n0, s0, n, q, slot):
+            nc.scalar.copy(out=gs_cols(0, 3, n0, s0, n), in_=spill_cols(pt, slot, n, q, 0, 3))
+            nc.scalar.copy(out=gs_cols(3, 4, n0, s0, n), in_=spill_cols(pt, slot - 1, n, q, 3, 4))
 
-        multiply(0, 0, 16, 0)
-        multiply(1, 12, 12, 128)
-        for s0 in (0, 2):
-            pt = psum.tile([P, 4, P], F32, tag="bank")
-            for slot in range(2):
-                strip(pt, slot, 12 + s0 + slot)
-            ptv = pt[:].rearrange("p (s u) (q c j) -> p q c s j u", s=2, q=4, c=4)
-            for q, n0 in ((0, 480), (1, 384)):
-                dst = gf[:, :, n0 + 8 * s0 : n0 + 8 * s0 + 16, :].rearrange("p c (s j) u -> p c s j u", s=2)
-                nc.scalar.copy(out=dst, in_=ptv[:, q])
-        for i in range(16, 24, 2):
+        def strip_bank(i):
             pt = psum.tile([P, 4, P], F32, tag="bank")
             for slot in range(2):
                 strip(pt, slot, i + slot)
-            ptv = pt[:].rearrange("p (s u) (q c j) -> p q c s j u", s=2, q=4, c=4)
-            n0 = 384 + 8 * (i - 12)
-            dst = gf[:, :, n0 : n0 + 16, :].rearrange("p c (s j) u -> p c s j u", s=2)
-            copy_out("v" if i % 4 == 0 else "s", dst, ptv[:, 1])
+            return pt[:].rearrange("p (s u) (q c j) -> p q c j s u", s=2, q=4, c=4)
+
+        def group_cols(h, a):
+            if h < 2:
+                return g_cols(96 * h, 12, a)
+            return g_cols(192 + 64 * (h - 2), 8, a) if a < 8 else g_cols(384 + 32 * (h - 2), 4, a - 8)
+
+        multiply(0, 0, 16, 0)
+        multiply(1, 12, 12, 128)
+        for i in range(12, 24, 2):
+            ptv = strip_bank(i)
+            if i < 16:
+                nc.scalar.copy(out=g_cols(480, 4, i - 12), in_=ptv[:, 0])
+            copy_out("v" if i % 4 == 0 else "s", group_cols(4, i - 12), ptv[:, 1])
         pt = psum.tile([P, 4, P], F32, tag="bank")
         for slot in range(4):
             spill(pt, slot, 12 + slot)
-        nc.scalar.copy(out=gs_cols(0, 3, 224, 4), in_=spill_cols(pt, 0, 4, 0, 0, 3))
-        nc.scalar.copy(out=gs_cols(3, 4, 232, 3), in_=spill_cols(pt, 0, 3, 0, 3, 4))
+        nc.scalar.copy(out=gs_cols(0, 3, 96, 0, 4), in_=spill_cols(pt, 0, 4, 0, 0, 3))
+        nc.scalar.copy(out=gs_cols(3, 4, 96, 1, 3), in_=spill_cols(pt, 0, 3, 0, 3, 4))
         pt = psum.tile([P, 4, P], F32, tag="bank")
         for slot in range(4):
             spill(pt, slot, 20 + slot)
-        spill_copy(pt, 200, 3, 1, 1)
+        spill_copy(pt, 64, 1, 3, 1, 1)
         multiply(1, 0, 12, 32)
         multiply(2, 0, 12, 64)
         multiply(3, 0, 12, 96)
         pt = psum.tile([P, 4, P], F32, tag="bank")
         for slot in range(3):
             spill(pt, slot, 9 + slot)
-        spill_copy(pt, 24, 1, 2, 2)
-        spill_copy(pt, 112, 2, 3, 1)
-        nc.scalar.copy(out=gs_cols(3, 4, 224, 1), in_=spill_cols(pt, 2, 1, 0, 3, 4))
+        spill_copy(pt, 0, 3, 1, 2, 2)
+        spill_copy(pt, 32, 2, 2, 3, 1)
+        nc.scalar.copy(out=gs_cols(3, 4, 96, 0, 1), in_=spill_cols(pt, 2, 1, 0, 3, 4))
         for i in range(0, 12, 2):
-            pt = psum.tile([P, 4, P], F32, tag="bank")
-            for slot in range(2):
-                strip(pt, slot, i + slot)
-            for slot in range(2):
-                dst = gf[:, :, 0:384, :].rearrange("p c (h a j) u -> p h c a j u", h=4, a=12)
-                copy_out(
-                    "s" if i % 4 == 0 else "v",
-                    dst[:, :, :, i + slot],
-                    pt[:, 2 * slot : 2 * slot + 2, :].rearrange("p u (h c j) -> p h c j u", h=4, c=4),
-                )
+            ptv = strip_bank(i)
+            for h in range(4):
+                copy_out("s" if i % 4 == 0 else "v", group_cols(h, i), ptv[:, h])
         quantise_w(0)
-        quantise_spill(0)
-        quantise_w(1)
+        quantise_spill()
 
-        for pair in range(MT // 2):
-            ta, tb = 2 * pair, 2 * pair + 1
-            o_a = outp.tile([P, O + 256], F32, tag="o_sb")
-            o_b = outp.tile([P, O + 256], F32, tag="o_sb")
-            last = pair == MT // 2 - 1
-            for c in range(4):
-                acc_b = passes(tb, c)
-                acc_a = passes(ta, c)
-                if c == 3 and not last:
-                    quantise_x(ta + 2)
-                evict(acc_b, o_b, c, False)
-                evict(acc_a, o_a, c, not last)
-                if pair == 0 and c == 0:
-                    quantise_spill(1)
-                    quantise_w(2)
-                if pair == 0 and c == 1:
-                    quantise_w(3)
-                if c < 2 and not last:
-                    for h in range(2):
-                        x_bank(ta + 2 + c, h, "s")
-            if not last:
-                quantise_x(tb + 2)
-            nc.sync.dma_start(out=out[tb * P : (tb + 1) * P, :], in_=o_b[:, 0:O])
+        by_s = [(mt, c) for mt in S_TILES for c in range(4)]
+        by_v = [(mt, c) for mt in range(MT) if mt not in S_TILES for c in range(4)]
+        o_of = {}
+
+        def product(mt, c, by_scalar):
+            if c == 0:
+                o_sb = outp.tile([P, O + 256], F32, tag="o_sb")
+                o_of[mt] = o_sb
+            evict(passes(mt, c), o_of[mt], c, by_scalar)
+            if c < 3:
+                return
+            o_sb = o_of[mt]
+            if not by_scalar:
+                nc.sync.dma_start(out=out[mt * P : (mt + 1) * P, :], in_=o_sb[:, 0:O])
+                return
+            for half in range(2):
+                o_half = o_sb[:, 1024 * half : 1024 * half + 1024]
+                nc.gpsimd.tensor_tensor(out=o_half, in0=o_half, in1=bias_bc[:, 1024 * half : 1024 * half + 1024], op=ADD)
+
+        def store_s(mt):
             for half in range(2):
                 lo = 1024 * half
-                o_half = o_a[:, lo : lo + 1024]
-                if not last:
-                    nc.gpsimd.tensor_tensor(out=o_half, in0=o_half, in1=bias_bc[:, lo : lo + 1024], op=ADD)
-                nc.sync.dma_start(out=out[ta * P : (ta + 1) * P, lo : lo + 1024], in_=o_half)
+                nc.sync.dma_start(out=out[mt * P : (mt + 1) * P, lo : lo + 1024], in_=o_of[mt][:, lo : lo + 1024])
+
+        for n in range(len(by_v)):
+            k, i = n // 4, n % 4
+            if n < len(by_s):
+                product(*by_s[n], True)
+            if n < 3:
+                quantise_w(n + 1)
+            if n < len(by_s) and i == 3:
+                quantise_x(2 * k + 2)
+            product(*by_v[n], False)
+            if n < len(by_s):
+                if i == 0 or i == 2:
+                    mt = 2 * k + 2 + i // 2
+                    x_bank(mt, 0, "s")
+                    x_bank(mt, 1, "v" if i == 0 else "s")
+                if i == 3:
+                    quantise_x(2 * k + 3)
+            if i == 3 and 1 <= k <= len(S_TILES):
+                store_s(S_TILES[k - 1])

@@ -41,11 +41,11 @@ def tile_structuredconnection_kernel(tc, x, weight, bias, mask, out):
         ma = keep.tile([P, STRIPS, L], BF16)
         z = keep.tile([P, ZW], BF16, align_bytes=64)
         g = keep.tile([P, 8192], BF16, align_bytes=64)
-        gs = keep.tile([P, 2048], BF16, align_bytes=64)
+        gs = keep.tile([P, 4096], BF16, align_bytes=64)
         wq = keep.tile([P, 2048], U32, align_bytes=64)
         ws = keep.tile([P, 2048], U8, align_bytes=64)
-        wsq = keep.tile([P, 512], U32, align_bytes=64)
-        wss = keep.tile([P, 512], U8, align_bytes=64)
+        wsq = keep.tile([P, 1024], U32, align_bytes=64)
+        wss = keep.tile([P, 1024], U8, align_bytes=64)
         x_sb = keep.tile([P, MT * K], BF16, align_bytes=64)
         xq = keep.tile([P, MT * 512], U32, align_bytes=64)
         xs = keep.tile([P, MT * 512], U8, align_bytes=64)
@@ -63,13 +63,13 @@ def tile_structuredconnection_kernel(tc, x, weight, bias, mask, out):
         wj = weight.rearrange("(j r) k -> j (r k)", j=8)
         mj = mask.rearrange("(j r) k -> j (r k)", j=8)
 
-        def load(src, dst, p0, d0, row, col, n, i0, i1):
+        def load(queue, src, dst, p0, d0, row, col, n, i0, i1):
             s0 = row * K + col
             if n == 1:
-                nc.sync.dma_start(out=dst[p0 : p0 + 8, d0, i0:i1], in_=src[:, s0 + i0 : s0 + i1])
+                queue.dma_start(out=dst[p0 : p0 + 8, d0, i0:i1], in_=src[:, s0 + i0 : s0 + i1])
             else:
                 rows = src[:, s0 : s0 + n * ROWSTEP].rearrange("j (a w) -> j a w", w=ROWSTEP)
-                nc.sync.dma_start(out=dst[p0 : p0 + 8, d0 : d0 + n, i0:i1], in_=rows[:, :, i0:i1])
+                queue.dma_start(out=dst[p0 : p0 + 8, d0 : d0 + n, i0:i1], in_=rows[:, :, i0:i1])
 
         def load_x(t0):
             nc.sync.dma_start(
@@ -83,31 +83,27 @@ def tile_structuredconnection_kernel(tc, x, weight, bias, mask, out):
                 col = 512 * c + 32 * h - 24
                 p0 = 32 * (h % 4) + 8 * c if h < 4 else 32 + 8 * c
                 d0 = 0 if h < 4 else 12
-                for src, dst in ((wj, wa), (mj, ma)):
+                for queue, src, dst in ((nc.sync, wj, wa), (nc.scalar, mj, ma)):
                     if h == 0 and c == 0:
-                        load(src, dst, p0, 1, row + 1, col + 40, 15, 0, L)
-                        load(src, dst, p0, 0, row, col, 1, 24, L)
+                        load(queue, src, dst, p0, 1, row + 1, col + 40, 15, 0, L)
+                        load(queue, src, dst, p0, 0, row, col, 1, 24, L)
                     elif h == 1 and c == 3:
-                        load(src, dst, p0, 0, row, col, 11, 0, L)
-                        load(src, dst, p0, 11, row + 11, col + 440, 1, 0, 64)
+                        load(queue, src, dst, p0, 0, row, col, 11, 0, L)
+                        load(queue, src, dst, p0, 11, row + 11, col + 440, 1, 0, 64)
                     else:
-                        load(src, dst, p0, d0, row, col, 16 if h == 0 else 12, 0, L)
+                        load(queue, src, dst, p0, d0, row, col, 16 if h == 0 else 12, 0, L)
 
         load_x(0)
-        load_h(0)
-        load_h(4)
-        load_h(1)
-        load_h(2)
-        load_h(3)
+        for h in (0, 4, 1, 2, 3):
+            load_h(h)
         load_x(2)
         load_x(4)
         load_x(6)
         nc.gpsimd.memset(bz[:].bitcast(F32), 0.0)
-        nc.scalar.dma_start(out=bz[0:1, :], in_=bias.rearrange("(o n) -> o n", o=1))
-
+        nc.gpsimd.dma_start(out=bz[0:1, :], in_=bias.rearrange("(o n) -> o n", o=1))
+        nc.gpsimd.memset(ones[:], 1.0)
         zhalf = FRONT + 12 * S
         nc.vector.memset(z[:, 0:zhalf].bitcast(I32), 0)
-        nc.gpsimd.memset(ones[:], 1.0)
         nc.gpsimd.memset(z[:, zhalf:ZLIVE].bitcast(F32), 0.0)
         nc.gpsimd.memset(gs[:].bitcast(F32), 0.0)
 
@@ -149,8 +145,12 @@ def tile_structuredconnection_kernel(tc, x, weight, bias, mask, out):
                 in_=g[:, 2048 * c : 2048 * c + 2048],
             )
 
-        def quantise_spill():
-            nc.vector.quantize_mx(out=wsq[:].bitcast(FP8X4), scales=wss[:], in_=gs[:])
+        def quantise_spill(half):
+            nc.vector.quantize_mx(
+                out=wsq[:, 512 * half : 512 * half + 512].bitcast(FP8X4),
+                scales=wss[:, 512 * half : 512 * half + 512],
+                in_=gs[:, 2048 * half : 2048 * half + 2048],
+            )
 
         xg_of = {}
 
@@ -180,60 +180,54 @@ def tile_structuredconnection_kernel(tc, x, weight, bias, mask, out):
         def passes(mt, c):
             acc = psum.tile([P, 512], F32, tag="bank")
             lhs, lhs_s = x_operand(mt, c)
-            for n0, n1 in ((0, 256), (256, 384), (384, 512)):
-                lo, hi = 512 * c + n0, 512 * c + n1
+            for n0 in (0, 256):
+                lo = 512 * c + n0
                 nc.tensor.matmul_mx(
-                    out=acc[:, n0:n1],
+                    out=acc[:, n0 : n0 + 256],
                     lhsT=lhs,
                     lhsT_scale=lhs_s,
-                    rhs=wq[:, lo:hi].bitcast(FP8X4),
-                    rhs_scale=ws[:, lo:hi],
+                    rhs=wq[:, lo : lo + 256].bitcast(FP8X4),
+                    rhs_scale=ws[:, lo : lo + 256],
                     start=True,
-                    stop=(n1 < 512),
+                    stop=(n0 == 0),
                 )
             lhs, lhs_s = x_operand(mt, (c + 1) % 4)
             nc.tensor.matmul_mx(
-                out=acc[:, 384:512],
+                out=acc[:, 256:512],
                 lhsT=lhs,
                 lhsT_scale=lhs_s,
-                rhs=wsq[:, 128 * c : 128 * c + 128].bitcast(FP8X4),
-                rhs_scale=wss[:, 128 * c : 128 * c + 128],
+                rhs=wsq[:, 256 * c : 256 * c + 256].bitcast(FP8X4),
+                rhs_scale=wss[:, 256 * c : 256 * c + 256],
                 start=False,
                 stop=True,
             )
             return acc
 
-        def out_runs(t, c, h0, nh, a0, na):
-            b0 = (64 * c + 52 * h0) % 256
-            v = t[:, b0 : b0 + 2048].rearrange("p (j r) -> p j r", r=256)
-            if nh == 1:
-                return v[:, :, a0 : a0 + na]
-            return v[:, :, 0 : 52 * nh].rearrange("p j (h e) -> p j h e", e=52)[:, :, :, a0 : a0 + na]
+        def out_runs(t, b0, nh):
+            v = t[:, b0 : b0 + 2048].rearrange("p (j r) -> p j r", r=256)[:, :, 0 : 52 * nh]
+            return v.rearrange("p j (h e) -> p j h e", e=52)[:, :, :, 0:12]
 
-        def sum_cols(acc, n0, nh, na):
-            v = acc[:, n0 : n0 + 8 * nh * na]
-            if nh == 1:
-                return v.rearrange("p (j a) -> p j a", j=8)
-            return v.rearrange("p (h j a) -> p j h a", h=nh, j=8)
+        def leave(by_scalar, dst, src, b):
+            if by_scalar:
+                nc.scalar.copy(out=dst, in_=src)
+            else:
+                nc.vector.tensor_tensor(out=dst, in0=src, in1=b, op=ADD)
 
         def evict(acc, o_sb, c, by_scalar):
-            wrap = (5, 4, 3, 2)[c]
-            parts = [(0, 0, 2, 0, 12)]
-            for h0, h1 in ((2, wrap), (wrap, 5)):
-                if h0 < h1:
-                    parts.append((192 + 64 * (h0 - 2), h0, h1 - h0, 0, 8))
-                    parts.append((384 + 32 * (h0 - 2), h0, h1 - h0, 8, 4))
-            parts.append((480, 0, 1, 12, 4))
-            for n0, h0, nh, a0, na in parts:
-                dst, src = out_runs(o_sb, c, h0, nh, a0, na), sum_cols(acc, n0, nh, na)
-                if by_scalar:
-                    nc.scalar.copy(out=dst, in_=src)
-                else:
-                    nc.vector.tensor_tensor(out=dst, in0=src, in1=out_runs(bias_bc, c, h0, nh, a0, na), op=ADD)
+            pa = acc[:, 0:480].rearrange("p (h a j) -> p j h a", h=5, a=12)
+            split = (4, 4, 3, 2)[c]
+            for h0, h1 in ((0, split), (split, 5)):
+                b0 = (64 * c + 52 * h0) % 256
+                leave(by_scalar, out_runs(o_sb, b0, h1 - h0), pa[:, :, h0:h1, :], out_runs(bias_bc, b0, h1 - h0))
+            pb = acc[:, 480:512].rearrange("p (s j) -> p j s", s=4)
+            b0 = 64 * c + 12
+            o_run = o_sb[:, b0 : b0 + 2048].rearrange("p (j r) -> p j r", r=256)[:, :, 0:4]
+            b_run = bias_bc[:, b0 : b0 + 2048].rearrange("p (j r) -> p j r", r=256)[:, :, 0:4]
+            leave(by_scalar, o_run, pb, b_run)
 
         for mt in range(2):
             for h in range(2):
-                x_bank(mt, h, "v" if h == 1 else "s")
+                x_bank(mt, h, "v")
             quantise_x(mt)
 
         for n in range(4):
@@ -241,65 +235,67 @@ def tile_structuredconnection_kernel(tc, x, weight, bias, mask, out):
             nc.tensor.matmul(bps[:], lhsT=ones[:], rhs=bz[:, 512 * n : 512 * n + 512], start=True, stop=True)
             nc.scalar.copy(out=bias_bc[:, 512 * n : 512 * n + 512], in_=bps[:])
 
-        def g_cols(n0, pitch, a):
-            v = gf[:, :, n0 : n0 + 8 * pitch, :].rearrange("p c (j a) u -> p c j a u", j=8)
-            return v[:, :, :, a : a + 2, :]
+        def gs_cols(c0, c1, n0, n):
+            return gsf[0:64, c0:c1, n0 : n0 + 8 * n, 0].rearrange("p c (s j) -> p c s j", s=n)
 
-        def gs_cols(c0, c1, n0, s0, n):
-            v = gsf[0:64, c0:c1, n0 : n0 + 32, 0].rearrange("p c (j s) -> p c j s", s=4)
-            return v[:, :, :, s0 : s0 + n]
-
-        def spill_cols(pt, slot, n, q, c0, c1):
+        def spill_cols(pt, s0, n, q, c0, c1):
             lo = 32 * q + 8 * c0
-            src = pt[0:64, slot : slot + n, lo : lo + 8 * (c1 - c0)]
-            return src.rearrange("p s (c j) -> p c j s", c=c1 - c0)
+            src = pt[0:64, s0 : s0 + n, lo : lo + 8 * (c1 - c0)]
+            return src.rearrange("p s (c j) -> p c s j", c=c1 - c0)
 
-        def spill_copy(pt, n0, s0, n, q, slot):
-            nc.scalar.copy(out=gs_cols(0, 3, n0, s0, n), in_=spill_cols(pt, slot, n, q, 0, 3))
-            nc.scalar.copy(out=gs_cols(3, 4, n0, s0, n), in_=spill_cols(pt, slot - 1, n, q, 3, 4))
-
-        def strip_bank(i):
-            pt = psum.tile([P, 4, P], F32, tag="bank")
-            for slot in range(2):
-                strip(pt, slot, i + slot)
-            return pt[:].rearrange("p (s u) (q c j) -> p q c j s u", s=2, q=4, c=4)
-
-        def group_cols(h, a):
-            if h < 2:
-                return g_cols(96 * h, 12, a)
-            return g_cols(192 + 64 * (h - 2), 8, a) if a < 8 else g_cols(384 + 32 * (h - 2), 4, a - 8)
+        def spill_copy(pt, n0, n, q, slot):
+            nc.scalar.copy(out=gs_cols(0, 3, n0, n), in_=spill_cols(pt, slot, n, q, 0, 3))
+            nc.scalar.copy(out=gs_cols(3, 4, n0, n), in_=spill_cols(pt, slot - 1, n, q, 3, 4))
 
         multiply(0, 0, 16, 0)
         multiply(1, 12, 12, 128)
-        for i in range(12, 24, 2):
-            ptv = strip_bank(i)
-            if i < 16:
-                nc.scalar.copy(out=g_cols(480, 4, i - 12), in_=ptv[:, 0])
-            copy_out("v" if i % 4 == 0 else "s", group_cols(4, i - 12), ptv[:, 1])
+        for s0 in (0, 2):
+            pt = psum.tile([P, 4, P], F32, tag="bank")
+            for slot in range(2):
+                strip(pt, slot, 12 + s0 + slot)
+            ptv = pt[:].rearrange("p (s u) (q c j) -> p q c s j u", s=2, q=4, c=4)
+            for q, n0 in ((0, 480), (1, 384)):
+                dst = gf[:, :, n0 + 8 * s0 : n0 + 8 * s0 + 16, :].rearrange("p c (s j) u -> p c s j u", s=2)
+                nc.scalar.copy(out=dst, in_=ptv[:, q])
+        for i in range(16, 24, 2):
+            pt = psum.tile([P, 4, P], F32, tag="bank")
+            for slot in range(2):
+                strip(pt, slot, i + slot)
+            ptv = pt[:].rearrange("p (s u) (q c j) -> p q c s j u", s=2, q=4, c=4)
+            n0 = 384 + 8 * (i - 12)
+            dst = gf[:, :, n0 : n0 + 16, :].rearrange("p c (s j) u -> p c s j u", s=2)
+            copy_out("v" if i % 4 == 0 else "s", dst, ptv[:, 1])
         pt = psum.tile([P, 4, P], F32, tag="bank")
         for slot in range(4):
             spill(pt, slot, 12 + slot)
-        nc.scalar.copy(out=gs_cols(0, 3, 96, 0, 4), in_=spill_cols(pt, 0, 4, 0, 0, 3))
-        nc.scalar.copy(out=gs_cols(3, 4, 96, 1, 3), in_=spill_cols(pt, 0, 3, 0, 3, 4))
+        nc.scalar.copy(out=gs_cols(0, 3, 224, 4), in_=spill_cols(pt, 0, 4, 0, 0, 3))
+        nc.scalar.copy(out=gs_cols(3, 4, 232, 3), in_=spill_cols(pt, 0, 3, 0, 3, 4))
         pt = psum.tile([P, 4, P], F32, tag="bank")
         for slot in range(4):
             spill(pt, slot, 20 + slot)
-        spill_copy(pt, 64, 1, 3, 1, 1)
+        spill_copy(pt, 200, 3, 1, 1)
         multiply(1, 0, 12, 32)
         multiply(2, 0, 12, 64)
         multiply(3, 0, 12, 96)
         pt = psum.tile([P, 4, P], F32, tag="bank")
         for slot in range(3):
             spill(pt, slot, 9 + slot)
-        spill_copy(pt, 0, 3, 1, 2, 2)
-        spill_copy(pt, 32, 2, 2, 3, 1)
-        nc.scalar.copy(out=gs_cols(3, 4, 96, 0, 1), in_=spill_cols(pt, 2, 1, 0, 3, 4))
+        spill_copy(pt, 24, 1, 2, 2)
+        spill_copy(pt, 112, 2, 3, 1)
+        nc.scalar.copy(out=gs_cols(3, 4, 224, 1), in_=spill_cols(pt, 2, 1, 0, 3, 4))
         for i in range(0, 12, 2):
-            ptv = strip_bank(i)
-            for h in range(4):
-                copy_out("s" if i % 4 == 0 else "v", group_cols(h, i), ptv[:, h])
+            pt = psum.tile([P, 4, P], F32, tag="bank")
+            for slot in range(2):
+                strip(pt, slot, i + slot)
+            for slot in range(2):
+                dst = gf[:, :, 0:384, :].rearrange("p c (h a j) u -> p h c a j u", h=4, a=12)
+                copy_out(
+                    "s" if i % 4 == 0 else "v",
+                    dst[:, :, :, i + slot],
+                    pt[:, 2 * slot : 2 * slot + 2, :].rearrange("p u (h c j) -> p h c j u", h=4, c=4),
+                )
         quantise_w(0)
-        quantise_spill()
+        quantise_spill(0)
 
         by_s = [(mt, c) for mt in S_TILES for c in range(4)]
         by_v = [(mt, c) for mt in range(MT) if mt not in S_TILES for c in range(4)]
@@ -331,6 +327,8 @@ def tile_structuredconnection_kernel(tc, x, weight, bias, mask, out):
                 product(*by_s[n], True)
             if n < 3:
                 quantise_w(n + 1)
+            if n == 0:
+                quantise_spill(1)
             if n < len(by_s) and i == 3:
                 quantise_x(2 * k + 2)
             product(*by_v[n], False)

@@ -15,102 +15,71 @@ MULT = mybir.AluOpType.mult
 P = 128
 M, K, O = 1024, 2048, 2048
 MT = M // P
-S_TILES = (0, 2, 4)
 FLOPS = 2 * M * O * 64
 BYTES = M * K * 2 + M * O * 4 + 2 * O * 64 * 2 + O * 2
+S_TILES = (0, 2, 4)
+EARLY = 4
 
-S = 704
-FRONT = 32
-L = 128
-STRIPS = 24
-ZLIVE = FRONT + S * (STRIPS - 1) + 768
-ZW = FRONT + S * STRIPS + 640
-ROWSTEP = K + 40
+RUNS = 16
+WIN = 640
+ZWIN = 1024
 
 
 def tile_structuredconnection_kernel(tc, x, weight, bias, mask, out):
     nc = tc.nc
     with ExitStack() as ctx:
         keep = ctx.enter_context(tc.tile_pool(name="keep", bufs=1))
-        xgp = ctx.enter_context(tc.tile_pool(name="xgp", bufs=3))
+        wp = ctx.enter_context(tc.tile_pool(name="wp", bufs=8))
+        gp = ctx.enter_context(tc.tile_pool(name="gp", bufs=4))
         outp = ctx.enter_context(tc.tile_pool(name="outp", bufs=6))
         psum = ctx.enter_context(tc.psum_pool(name="psum", bufs=8))
         ctx.enter_context(tc.manual_schedule())
 
-        wa = keep.tile([P, STRIPS, L], BF16)
-        ma = keep.tile([P, STRIPS, L], BF16)
-        z = keep.tile([P, ZW], BF16, align_bytes=64)
-        g = keep.tile([P, 8192], BF16, align_bytes=64)
-        gs = keep.tile([P, 4096], BF16, align_bytes=64)
-        wq = keep.tile([P, 2048], U32, align_bytes=64)
-        ws = keep.tile([P, 2048], U8, align_bytes=64)
-        wsq = keep.tile([P, 1024], U32, align_bytes=64)
-        wss = keep.tile([P, 1024], U8, align_bytes=64)
-        x_sb = keep.tile([P, MT * K], BF16, align_bytes=64)
+        zt = keep.tile([P, RUNS, ZWIN], BF16, align_bytes=64)
+        wq = keep.tile([P, RUNS * 256], U32, align_bytes=64)
+        ws = keep.tile([P, RUNS * 256], U8, align_bytes=64)
+        x_sb = keep.tile([P, MT, K], BF16, align_bytes=64)
         xq = keep.tile([P, MT * 512], U32, align_bytes=64)
         xs = keep.tile([P, MT * 512], U8, align_bytes=64)
         ident = keep.tile([P, P], F32)
         ones = keep.tile([P, P], BF16)
         bz = keep.tile([P, O], BF16)
-        bias_bc = keep.tile([P, O + 256], F32)
+        bias_bc = keep.tile([P, O], F32)
 
-        nc.vector.memset(wa[0:32, 0, 0:32], 0.0)
-        nc.vector.memset(ma[0:32, 0, 0:32], 0.0)
-        nc.vector.memset(wa[32:64, 11, 64:L], 0.0)
-        nc.vector.memset(ma[32:64, 11, 64:L], 0.0)
         make_identity(nc, ident[:])
-
-        wj = weight.rearrange("(j r) k -> j (r k)", j=8)
-        mj = mask.rearrange("(j r) k -> j (r k)", j=8)
-
-        def load(queue, src, dst, p0, d0, row, col, n, i0, i1):
-            s0 = row * K + col
-            if n == 1:
-                queue.dma_start(out=dst[p0 : p0 + 8, d0, i0:i1], in_=src[:, s0 + i0 : s0 + i1])
-            else:
-                rows = src[:, s0 : s0 + n * ROWSTEP].rearrange("j (a w) -> j a w", w=ROWSTEP)
-                queue.dma_start(out=dst[p0 : p0 + 8, d0 : d0 + n, i0:i1], in_=rows[:, :, i0:i1])
-
-        def load_x(t0):
-            nc.sync.dma_start(
-                out=x_sb[:, t0 * K : (t0 + 2) * K].rearrange("p (t k) -> p t k", t=2),
-                in_=x[t0 * P : (t0 + 2) * P, :].rearrange("(t p) k -> p t k", p=P),
-            )
-
-        def load_h(h):
-            for c in range(4):
-                row = (64 * c + 52 * h) % 256
-                col = 512 * c + 32 * h - 24
-                p0 = 32 * (h % 4) + 8 * c if h < 4 else 32 + 8 * c
-                d0 = 0 if h < 4 else 12
-                for queue, src, dst in ((nc.sync, wj, wa), (nc.scalar, mj, ma)):
-                    if h == 0 and c == 0:
-                        load(queue, src, dst, p0, 1, row + 1, col + 40, 15, 0, L)
-                        load(queue, src, dst, p0, 0, row, col, 1, 24, L)
-                    elif h == 1 and c == 3:
-                        load(queue, src, dst, p0, 0, row, col, 11, 0, L)
-                        load(queue, src, dst, p0, 11, row + 11, col + 440, 1, 0, 64)
-                    else:
-                        load(queue, src, dst, p0, d0, row, col, 16 if h == 0 else 12, 0, L)
-
-        load_x(0)
-        for h in (0, 4, 1, 2, 3):
-            load_h(h)
-        load_x(2)
-        load_x(4)
-        load_x(6)
         nc.gpsimd.memset(bz[:].bitcast(F32), 0.0)
-        nc.gpsimd.dma_start(out=bz[0:1, :], in_=bias.rearrange("(o n) -> o n", o=1))
+        nc.scalar.dma_start(out=bz[0:1, :], in_=bias.rearrange("(o n) -> o n", o=1))
         nc.gpsimd.memset(ones[:], 1.0)
-        zhalf = FRONT + 12 * S
-        nc.vector.memset(z[:, 0:zhalf].bitcast(I32), 0)
-        nc.gpsimd.memset(z[:, zhalf:ZLIVE].bitcast(F32), 0.0)
-        nc.gpsimd.memset(gs[:].bitcast(F32), 0.0)
 
-        zf = z[:].bitcast(F32)
-        gf = g[:].bitcast(F32).rearrange("p (c n u) -> p c n u", c=4, u=2)
-        gsf = gs[:].bitcast(F32).rearrange("p (c n u) -> p c n u", c=4, u=2)
-        xf = x_sb[:].bitcast(F32)
+        wt = weight.rearrange("(j t a) k -> t a j k", j=8, t=RUNS)
+        mk = mask.rearrange("(j t a) k -> t a j k", j=8, t=RUNS)
+
+        loaded = {}
+
+        def load_run(t):
+            col = (640 * t) % K
+            first = min(WIN, K - col)
+            tiles = []
+            for src, name in ((wt, "w_run"), (mk, "m_run")):
+                tile = wp.tile([P, WIN], BF16, tag=name, name=name)
+                nc.sync.dma_start(out=tile[:, 0:first], in_=src[t, :, :, col : col + first])
+                if first < WIN:
+                    nc.sync.dma_start(out=tile[:, first:WIN], in_=src[t, :, :, 0 : WIN - first])
+                tiles.append(tile)
+            loaded[t] = tiles
+
+        def load_x(mt):
+            nc.sync.dma_start(out=x_sb[:, mt, :], in_=x[mt * P : (mt + 1) * P, :])
+
+        zf = zt[:].rearrange("p t w -> p (t w)").bitcast(F32)
+        zi = zt[:].rearrange("p t w -> p (t w)").bitcast(I32).rearrange("p (t w) -> p t w", t=RUNS)
+        xf = x_sb[:].rearrange("p t k -> p (t k)").bitcast(F32)
+
+        for r in range(4):
+            if r > 0:
+                nc.vector.memset(zi[:, r:RUNS:4, 0 : 64 * r], 0)
+            if r < 3:
+                nc.vector.memset(zi[:, r:RUNS:4, 64 * r + WIN // 2 : ZWIN // 2], 0)
 
         def copy_out(engine, dst, src):
             if engine == "s":
@@ -118,53 +87,45 @@ def tile_structuredconnection_kernel(tc, x, weight, bias, mask, out):
             else:
                 nc.vector.tensor_copy(out=dst, in_=src)
 
-        def strip(pt, slot, i):
-            for uh in range(2):
-                w0 = (FRONT + S * i + 256 * uh) // 2
-                nc.tensor.transpose(pt[:, 2 * slot + uh, :], zf[:, w0 : w0 + P], ident[:])
+        def multiply(t):
+            d0 = 128 * (t % 4)
+            w_run, m_run = loaded[t]
+            nc.vector.tensor_tensor(out=zt[:, t, d0 : d0 + WIN], in0=w_run[:], in1=m_run[:], op=MULT)
 
-        def spill(pt, slot, i):
-            w0 = (FRONT + S * i + 512) // 2
-            nc.tensor.transpose(pt[:, slot, :], zf[:, w0 : w0 + P], ident[:])
+        g_of = {}
 
-        def multiply(q, i0, n, off):
-            p0 = 32 * q
-            s0 = FRONT + S * i0 + off - 24
-            dst = z[p0 : p0 + 32, s0 : s0 + n * (S + 40)].rearrange("p (a w) -> p a w", w=S + 40)
-            nc.vector.tensor_tensor(
-                out=dst[:, :, 0:L],
-                in0=wa[p0 : p0 + 32, i0 : i0 + n, :],
-                in1=ma[p0 : p0 + 32, i0 : i0 + n, :],
-                op=MULT,
-            )
+        def turn_run(t, engine):
+            if t % 2 == 0:
+                g = gp.tile([P, 2048], BF16, align_bytes=64, tag="g")
+                g_of[t // 2] = g
+            gf = g_of[t // 2][:].bitcast(F32).rearrange("p (r b j a u) -> p r b j a u", r=2, b=2, j=8, u=2)
+            pt = psum.tile([P, 4, P], F32, tag="bank")
+            for k in range(4):
+                w0 = t * (ZWIN // 2) + P * k
+                nc.tensor.transpose(pt[:, k, :], zf[:, w0 : w0 + P], ident[:])
+            src = pt[:].rearrange("p (b u) (a j) -> p b j a u", b=2, j=8)
+            for b in range(2):
+                copy_out(engine, gf[:, t % 2, b], src[:, b])
 
-        def quantise_w(c):
+        def quantise_runs(r):
             nc.vector.quantize_mx(
-                out=wq[:, 512 * c : 512 * c + 512].bitcast(FP8X4),
-                scales=ws[:, 512 * c : 512 * c + 512],
-                in_=g[:, 2048 * c : 2048 * c + 2048],
-            )
-
-        def quantise_spill(half):
-            nc.vector.quantize_mx(
-                out=wsq[:, 512 * half : 512 * half + 512].bitcast(FP8X4),
-                scales=wss[:, 512 * half : 512 * half + 512],
-                in_=gs[:, 2048 * half : 2048 * half + 2048],
+                out=wq[:, 512 * r : 512 * r + 512].bitcast(FP8X4),
+                scales=ws[:, 512 * r : 512 * r + 512],
+                in_=g_of[r][:],
             )
 
         xg_of = {}
 
-        def x_bank(mt, h, engine):
-            if h == 0:
-                xg = xgp.tile([P, 2048], BF16, align_bytes=64, tag="xg")
-                xg_of[mt] = xg
-            xg = xg_of[mt]
+        def turn_x(mt, engines):
+            xg = gp.tile([P, 2048], BF16, align_bytes=64, tag="g")
+            xg_of[mt] = xg
             xgf = xg[:].bitcast(F32).rearrange("p (c m u) -> p c m u", c=4, u=2)
-            pt = psum.tile([P, 4, P], F32, tag="bank")
-            for k in range(4):
-                w0 = mt * 1024 + 512 * h + 128 * k
-                nc.tensor.transpose(pt[:, k, :], xf[:, w0 : w0 + P], ident[:])
-            copy_out(engine, xgf[:, 2 * h : 2 * h + 2, :, :], pt[:].rearrange("p (c u) m -> p c m u", c=2))
+            for h in range(2):
+                pt = psum.tile([P, 4, P], F32, tag="bank")
+                for k in range(4):
+                    w0 = mt * 1024 + 512 * h + P * k
+                    nc.tensor.transpose(pt[:, k, :], xf[:, w0 : w0 + P], ident[:])
+                copy_out(engines[h], xgf[:, 2 * h : 2 * h + 2], pt[:].rearrange("p (c u) m -> p c m u", c=2))
 
         def quantise_x(mt):
             nc.vector.quantize_mx(
@@ -173,144 +134,72 @@ def tile_structuredconnection_kernel(tc, x, weight, bias, mask, out):
                 in_=xg_of[mt][:],
             )
 
-        def x_operand(mt, c):
-            lo = 512 * mt + 128 * c
-            return xq[:, lo : lo + 128].bitcast(FP8X4), xs[:, lo : lo + 128]
-
-        def passes(mt, c):
+        def sums(mt, b):
             acc = psum.tile([P, 512], F32, tag="bank")
-            lhs, lhs_s = x_operand(mt, c)
-            for n0 in (0, 256):
-                lo = 512 * c + n0
-                nc.tensor.matmul_mx(
-                    out=acc[:, n0 : n0 + 256],
-                    lhsT=lhs,
-                    lhsT_scale=lhs_s,
-                    rhs=wq[:, lo : lo + 256].bitcast(FP8X4),
-                    rhs_scale=ws[:, lo : lo + 256],
-                    start=True,
-                    stop=(n0 == 0),
-                )
-            lhs, lhs_s = x_operand(mt, (c + 1) % 4)
-            nc.tensor.matmul_mx(
-                out=acc[:, 256:512],
-                lhsT=lhs,
-                lhsT_scale=lhs_s,
-                rhs=wsq[:, 256 * c : 256 * c + 256].bitcast(FP8X4),
-                rhs_scale=wss[:, 256 * c : 256 * c + 256],
-                start=False,
-                stop=True,
-            )
+            for i in range(4):
+                t = 4 * b + i
+                c0 = 640 * t // 512
+                for part in range(2):
+                    c = (c0 + part) % 4
+                    lo, xo = 256 * t + 128 * part, 512 * mt + 128 * c
+                    nc.tensor.matmul_mx(
+                        out=acc[:, 128 * i : 128 * i + 128],
+                        lhsT=xq[:, xo : xo + 128].bitcast(FP8X4),
+                        lhsT_scale=xs[:, xo : xo + 128],
+                        rhs=wq[:, lo : lo + 128].bitcast(FP8X4),
+                        rhs_scale=ws[:, lo : lo + 128],
+                        start=(part == 0),
+                        stop=(part == 1),
+                    )
             return acc
 
-        def out_runs(t, b0, nh):
-            v = t[:, b0 : b0 + 2048].rearrange("p (j r) -> p j r", r=256)[:, :, 0 : 52 * nh]
-            return v.rearrange("p j (h e) -> p j h e", e=52)[:, :, :, 0:12]
-
-        def leave(by_scalar, dst, src, b):
+        def evict(acc, o_sb, b, by_scalar):
+            src = acc[:].rearrange("p (t j a) -> p j t a", t=4, j=8)
+            dst = o_sb[:].rearrange("p (j b t a) -> p b j t a", j=8, b=4, t=4)[:, b]
             if by_scalar:
                 nc.scalar.copy(out=dst, in_=src)
             else:
-                nc.vector.tensor_tensor(out=dst, in0=src, in1=b, op=ADD)
-
-        def evict(acc, o_sb, c, by_scalar):
-            pa = acc[:, 0:480].rearrange("p (h a j) -> p j h a", h=5, a=12)
-            split = (4, 4, 3, 2)[c]
-            for h0, h1 in ((0, split), (split, 5)):
-                b0 = (64 * c + 52 * h0) % 256
-                leave(by_scalar, out_runs(o_sb, b0, h1 - h0), pa[:, :, h0:h1, :], out_runs(bias_bc, b0, h1 - h0))
-            pb = acc[:, 480:512].rearrange("p (s j) -> p j s", s=4)
-            b0 = 64 * c + 12
-            o_run = o_sb[:, b0 : b0 + 2048].rearrange("p (j r) -> p j r", r=256)[:, :, 0:4]
-            b_run = bias_bc[:, b0 : b0 + 2048].rearrange("p (j r) -> p j r", r=256)[:, :, 0:4]
-            leave(by_scalar, o_run, pb, b_run)
-
-        for mt in range(2):
-            for h in range(2):
-                x_bank(mt, h, "v")
-            quantise_x(mt)
-
-        for n in range(4):
-            bps = psum.tile([P, 512], F32, tag="bank")
-            nc.tensor.matmul(bps[:], lhsT=ones[:], rhs=bz[:, 512 * n : 512 * n + 512], start=True, stop=True)
-            nc.scalar.copy(out=bias_bc[:, 512 * n : 512 * n + 512], in_=bps[:])
-
-        def gs_cols(c0, c1, n0, n):
-            return gsf[0:64, c0:c1, n0 : n0 + 8 * n, 0].rearrange("p c (s j) -> p c s j", s=n)
-
-        def spill_cols(pt, s0, n, q, c0, c1):
-            lo = 32 * q + 8 * c0
-            src = pt[0:64, s0 : s0 + n, lo : lo + 8 * (c1 - c0)]
-            return src.rearrange("p s (c j) -> p c s j", c=c1 - c0)
-
-        def spill_copy(pt, n0, n, q, slot):
-            nc.scalar.copy(out=gs_cols(0, 3, n0, n), in_=spill_cols(pt, slot, n, q, 0, 3))
-            nc.scalar.copy(out=gs_cols(3, 4, n0, n), in_=spill_cols(pt, slot - 1, n, q, 3, 4))
-
-        multiply(0, 0, 16, 0)
-        multiply(1, 12, 12, 128)
-        for s0 in (0, 2):
-            pt = psum.tile([P, 4, P], F32, tag="bank")
-            for slot in range(2):
-                strip(pt, slot, 12 + s0 + slot)
-            ptv = pt[:].rearrange("p (s u) (q c j) -> p q c s j u", s=2, q=4, c=4)
-            for q, n0 in ((0, 480), (1, 384)):
-                dst = gf[:, :, n0 + 8 * s0 : n0 + 8 * s0 + 16, :].rearrange("p c (s j) u -> p c s j u", s=2)
-                nc.scalar.copy(out=dst, in_=ptv[:, q])
-        for i in range(16, 24, 2):
-            pt = psum.tile([P, 4, P], F32, tag="bank")
-            for slot in range(2):
-                strip(pt, slot, i + slot)
-            ptv = pt[:].rearrange("p (s u) (q c j) -> p q c s j u", s=2, q=4, c=4)
-            n0 = 384 + 8 * (i - 12)
-            dst = gf[:, :, n0 : n0 + 16, :].rearrange("p c (s j) u -> p c s j u", s=2)
-            copy_out("v" if i % 4 == 0 else "s", dst, ptv[:, 1])
-        pt = psum.tile([P, 4, P], F32, tag="bank")
-        for slot in range(4):
-            spill(pt, slot, 12 + slot)
-        nc.scalar.copy(out=gs_cols(0, 3, 224, 4), in_=spill_cols(pt, 0, 4, 0, 0, 3))
-        nc.scalar.copy(out=gs_cols(3, 4, 232, 3), in_=spill_cols(pt, 0, 3, 0, 3, 4))
-        pt = psum.tile([P, 4, P], F32, tag="bank")
-        for slot in range(4):
-            spill(pt, slot, 20 + slot)
-        spill_copy(pt, 200, 3, 1, 1)
-        multiply(1, 0, 12, 32)
-        multiply(2, 0, 12, 64)
-        multiply(3, 0, 12, 96)
-        pt = psum.tile([P, 4, P], F32, tag="bank")
-        for slot in range(3):
-            spill(pt, slot, 9 + slot)
-        spill_copy(pt, 24, 1, 2, 2)
-        spill_copy(pt, 112, 2, 3, 1)
-        nc.scalar.copy(out=gs_cols(3, 4, 224, 1), in_=spill_cols(pt, 2, 1, 0, 3, 4))
-        for i in range(0, 12, 2):
-            pt = psum.tile([P, 4, P], F32, tag="bank")
-            for slot in range(2):
-                strip(pt, slot, i + slot)
-            for slot in range(2):
-                dst = gf[:, :, 0:384, :].rearrange("p c (h a j) u -> p h c a j u", h=4, a=12)
-                copy_out(
-                    "s" if i % 4 == 0 else "v",
-                    dst[:, :, :, i + slot],
-                    pt[:, 2 * slot : 2 * slot + 2, :].rearrange("p u (h c j) -> p h c j u", h=4, c=4),
+                nc.vector.tensor_tensor(
+                    out=dst, in0=src, in1=bias_bc[:].rearrange("p (j b t a) -> p b j t a", j=8, b=4, t=4)[:, b], op=ADD
                 )
-        quantise_w(0)
-        quantise_spill(0)
 
-        by_s = [(mt, c) for mt in S_TILES for c in range(4)]
-        by_v = [(mt, c) for mt in range(MT) if mt not in S_TILES for c in range(4)]
+        for t in range(RUNS):
+            load_run(t)
+            if t % 4 == 3 and t // 4 < EARLY:
+                load_x(t // 4)
+        for mt in range(EARLY, MT):
+            load_x(mt)
+        for step in range(RUNS + 5):
+            if step < RUNS:
+                multiply(step)
+            if 1 <= step <= RUNS:
+                turn_run(step - 1, "s")
+            if step >= 6 and (step - 6) % 4 == 0 and (step - 6) // 4 < EARLY:
+                turn_x((step - 6) // 4, "ss")
+            if step >= 4 and step % 2 == 0 and (step - 4) // 2 < RUNS // 2:
+                quantise_runs((step - 4) // 2)
+            if step >= 8 and (step - 8) % 4 == 0 and (step - 8) // 4 < EARLY:
+                quantise_x((step - 8) // 4)
+            if step == 1:
+                for n in range(4):
+                    bps = psum.tile([P, 512], F32, tag="bank")
+                    nc.tensor.matmul(bps[:], lhsT=ones[:], rhs=bz[:, 512 * n : 512 * n + 512], start=True, stop=True)
+                    nc.scalar.copy(out=bias_bc[:, 512 * n : 512 * n + 512], in_=bps[:])
+
+        by_s = [(mt, b) for mt in S_TILES for b in range(4)]
+        by_v = [(mt, b) for mt in range(MT) if mt not in S_TILES for b in range(4)]
         o_of = {}
 
-        def product(mt, c, by_scalar):
-            if c == 0:
-                o_sb = outp.tile([P, O + 256], F32, tag="o_sb")
+        def product(mt, b, by_scalar):
+            if b == 0:
+                o_sb = outp.tile([P, O], F32, tag="o_sb")
                 o_of[mt] = o_sb
-            evict(passes(mt, c), o_of[mt], c, by_scalar)
-            if c < 3:
+            evict(sums(mt, b), o_of[mt], b, by_scalar)
+            if b < 3:
                 return
             o_sb = o_of[mt]
             if not by_scalar:
-                nc.sync.dma_start(out=out[mt * P : (mt + 1) * P, :], in_=o_sb[:, 0:O])
+                nc.sync.dma_start(out=out[mt * P : (mt + 1) * P, :], in_=o_sb[:])
                 return
             for half in range(2):
                 o_half = o_sb[:, 1024 * half : 1024 * half + 1024]
@@ -322,22 +211,12 @@ def tile_structuredconnection_kernel(tc, x, weight, bias, mask, out):
                 nc.sync.dma_start(out=out[mt * P : (mt + 1) * P, lo : lo + 1024], in_=o_of[mt][:, lo : lo + 1024])
 
         for n in range(len(by_v)):
-            k, i = n // 4, n % 4
             if n < len(by_s):
                 product(*by_s[n], True)
-            if n < 3:
-                quantise_w(n + 1)
-            if n == 0:
-                quantise_spill(1)
-            if n < len(by_s) and i == 3:
-                quantise_x(2 * k + 2)
             product(*by_v[n], False)
-            if n < len(by_s):
-                if i == 0 or i == 2:
-                    mt = 2 * k + 2 + i // 2
-                    x_bank(mt, 0, "s")
-                    x_bank(mt, 1, "v" if i == 0 else "s")
-                if i == 3:
-                    quantise_x(2 * k + 3)
-            if i == 3 and 1 <= k <= len(S_TILES):
-                store_s(S_TILES[k - 1])
+            if n in (1, 3, 6, 8):
+                mt = {1: 4, 3: 5, 6: 6, 8: 7}[n]
+                turn_x(mt, "ss")
+                quantise_x(mt)
+            if n % 4 == 3 and 1 <= n // 4 <= len(S_TILES):
+                store_s(S_TILES[n // 4 - 1])

@@ -17,10 +17,10 @@ M, K, O = 1024, 2048, 2048
 MT = M // P
 FLOPS = 2 * M * O * 64
 BYTES = M * K * 2 + M * O * 4 + 2 * O * 64 * 2 + O * 2
-S_TILES = (0, 2, 4)
-EARLY = 4
+EARLY = 3
 
 RUNS = 16
+GROUPS = [[t for t in range(RUNS) if 5 * t // 4 % 4 == c] for c in range(4)]
 WIN = 640
 ZWIN = 1024
 
@@ -31,6 +31,7 @@ def tile_structuredconnection_kernel(tc, x, weight, bias, mask, out):
         keep = ctx.enter_context(tc.tile_pool(name="keep", bufs=1))
         wp = ctx.enter_context(tc.tile_pool(name="wp", bufs=8))
         gp = ctx.enter_context(tc.tile_pool(name="gp", bufs=4))
+        gwp = ctx.enter_context(tc.tile_pool(name="gwp", bufs=2))
         outp = ctx.enter_context(tc.tile_pool(name="outp", bufs=6))
         psum = ctx.enter_context(tc.psum_pool(name="psum", bufs=8))
         ctx.enter_context(tc.manual_schedule())
@@ -44,11 +45,14 @@ def tile_structuredconnection_kernel(tc, x, weight, bias, mask, out):
         ident = keep.tile([P, P], F32)
         ones = keep.tile([P, P], BF16)
         bz = keep.tile([P, O], BF16)
-        bias_bc = keep.tile([P, O], F32)
+        bias_bc = keep.tile([P, O + 256], F32)
 
         make_identity(nc, ident[:])
         nc.gpsimd.memset(bz[:].bitcast(F32), 0.0)
-        nc.scalar.dma_start(out=bz[0:1, :], in_=bias.rearrange("(o n) -> o n", o=1))
+        nc.gpsimd.dma_start(out=bz[0:1, :], in_=bias.rearrange("(o n) -> o n", o=1))
+        first = keep.tile([P, 1], F32)
+        nc.vector.memset(first[:], 0.0)
+        nc.scalar.copy(out=first[:], in_=first[:])
         nc.gpsimd.memset(ones[:], 1.0)
 
         wt = weight.rearrange("(j t a) k -> t a j k", j=8, t=RUNS)
@@ -94,38 +98,40 @@ def tile_structuredconnection_kernel(tc, x, weight, bias, mask, out):
 
         g_of = {}
 
-        def turn_run(t, engine):
-            if t % 2 == 0:
-                g = gp.tile([P, 2048], BF16, align_bytes=64, tag="g")
-                g_of[t // 2] = g
-            gf = g_of[t // 2][:].bitcast(F32).rearrange("p (r b j a u) -> p r b j a u", r=2, b=2, j=8, u=2)
+        def turn_run(c, i):
+            t = GROUPS[c][i]
+            if i == 0:
+                g = gwp.tile([P, 4096], BF16, align_bytes=64, tag="gw")
+                g_of[c] = g
+            gf = g_of[c][:].bitcast(F32).rearrange("p (b i j a u) -> p b i j a u", b=2, i=4, j=8, u=2)
             pt = psum.tile([P, 4, P], F32, tag="bank")
             for k in range(4):
                 w0 = t * (ZWIN // 2) + P * k
                 nc.tensor.transpose(pt[:, k, :], zf[:, w0 : w0 + P], ident[:])
             src = pt[:].rearrange("p (b u) (a j) -> p b j a u", b=2, j=8)
             for b in range(2):
-                copy_out(engine, gf[:, t % 2, b], src[:, b])
+                nc.scalar.copy(out=gf[:, b, i], in_=src[:, b])
 
-        def quantise_runs(r):
+        def quantise_part(c, b):
+            lo = 1024 * c + 512 * b
             nc.vector.quantize_mx(
-                out=wq[:, 512 * r : 512 * r + 512].bitcast(FP8X4),
-                scales=ws[:, 512 * r : 512 * r + 512],
-                in_=g_of[r][:],
+                out=wq[:, lo : lo + 512].bitcast(FP8X4),
+                scales=ws[:, lo : lo + 512],
+                in_=g_of[c][:, 2048 * b : 2048 * b + 2048],
             )
 
         xg_of = {}
 
-        def turn_x(mt, engines):
-            xg = gp.tile([P, 2048], BF16, align_bytes=64, tag="g")
-            xg_of[mt] = xg
-            xgf = xg[:].bitcast(F32).rearrange("p (c m u) -> p c m u", c=4, u=2)
-            for h in range(2):
-                pt = psum.tile([P, 4, P], F32, tag="bank")
-                for k in range(4):
-                    w0 = mt * 1024 + 512 * h + P * k
-                    nc.tensor.transpose(pt[:, k, :], xf[:, w0 : w0 + P], ident[:])
-                copy_out(engines[h], xgf[:, 2 * h : 2 * h + 2], pt[:].rearrange("p (c u) m -> p c m u", c=2))
+        def turn_x(mt, h, engine):
+            if h == 0:
+                xg = gp.tile([P, 2048], BF16, align_bytes=64, tag="g")
+                xg_of[mt] = xg
+            xgf = xg_of[mt][:].bitcast(F32).rearrange("p (c m u) -> p c m u", c=4, u=2)
+            pt = psum.tile([P, 4, P], F32, tag="bank")
+            for k in range(4):
+                w0 = mt * 1024 + 512 * h + P * k
+                nc.tensor.transpose(pt[:, k, :], xf[:, w0 : w0 + P], ident[:])
+            copy_out(engine, xgf[:, 2 * h : 2 * h + 2], pt[:].rearrange("p (c u) m -> p c m u", c=2))
 
         def quantise_x(mt):
             nc.vector.quantize_mx(
@@ -134,89 +140,93 @@ def tile_structuredconnection_kernel(tc, x, weight, bias, mask, out):
                 in_=xg_of[mt][:],
             )
 
-        def sums(mt, b):
+        def sums(mt, c):
             acc = psum.tile([P, 512], F32, tag="bank")
-            for i in range(4):
-                t = 4 * b + i
-                c0 = 640 * t // 512
-                for part in range(2):
-                    c = (c0 + part) % 4
-                    lo, xo = 256 * t + 128 * part, 512 * mt + 128 * c
-                    nc.tensor.matmul_mx(
-                        out=acc[:, 128 * i : 128 * i + 128],
-                        lhsT=xq[:, xo : xo + 128].bitcast(FP8X4),
-                        lhsT_scale=xs[:, xo : xo + 128],
-                        rhs=wq[:, lo : lo + 128].bitcast(FP8X4),
-                        rhs_scale=ws[:, lo : lo + 128],
-                        start=(part == 0),
-                        stop=(part == 1),
-                    )
+            for b in range(2):
+                lo, xo = 1024 * c + 512 * b, 512 * mt + 128 * ((c + b) % 4)
+                nc.tensor.matmul_mx(
+                    out=acc[:],
+                    lhsT=xq[:, xo : xo + 128].bitcast(FP8X4),
+                    lhsT_scale=xs[:, xo : xo + 128],
+                    rhs=wq[:, lo : lo + 512].bitcast(FP8X4),
+                    rhs_scale=ws[:, lo : lo + 512],
+                    start=(b == 0),
+                    stop=(b == 1),
+                )
             return acc
 
-        def evict(acc, o_sb, b, by_scalar):
-            src = acc[:].rearrange("p (t j a) -> p j t a", t=4, j=8)
-            dst = o_sb[:].rearrange("p (j b t a) -> p b j t a", j=8, b=4, t=4)[:, b]
-            if by_scalar:
-                nc.scalar.copy(out=dst, in_=src)
-            else:
-                nc.vector.tensor_tensor(
-                    out=dst, in0=src, in1=bias_bc[:].rearrange("p (j b t a) -> p b j t a", j=8, b=4, t=4)[:, b], op=ADD
-                )
+        def out_runs(t, b0, n):
+            v = t[:, b0 : b0 + 2048].rearrange("p (j r) -> p j r", r=256)[:, :, 0 : 48 * n]
+            return v.rearrange("p j (i e) -> p j i e", e=48)[:, :, :, 0:16]
 
-        for t in range(RUNS):
-            load_run(t)
-            if t % 4 == 3 and t // 4 < EARLY:
-                load_x(t // 4)
-        for mt in range(EARLY, MT):
+        def evict(acc, o_sb, c, j0, j1, by_scalar):
+            src = acc[:].rearrange("p (i j a) -> p j i a", i=4, j=8)
+            i0 = 0
+            while i0 < 4:
+                i1 = i0 + 1
+                while i1 < 4 and GROUPS[c][i1] == GROUPS[c][i1 - 1] + 3:
+                    i1 += 1
+                b0 = 16 * GROUPS[c][i0]
+                dst, b = out_runs(o_sb, b0, i1 - i0), out_runs(bias_bc, b0, i1 - i0)
+                if by_scalar:
+                    nc.scalar.copy(out=dst[:, j0:j1], in_=src[:, j0:j1, i0:i1])
+                else:
+                    nc.vector.tensor_tensor(
+                        out=dst[:, j0:j1], in0=src[:, j0:j1, i0:i1], in1=b[:, j0:j1], op=ADD
+                    )
+                i0 = i1
+
+        runs = [(c, i) for c in range(4) for i in range(4)]
+        for c, i in runs:
+            load_run(GROUPS[c][i])
+            if i == 3:
+                load_x(c)
+        for mt in range(4, MT):
             load_x(mt)
         for step in range(RUNS + 5):
             if step < RUNS:
-                multiply(step)
+                c, i = runs[step]
+                multiply(GROUPS[c][i])
             if 1 <= step <= RUNS:
-                turn_run(step - 1, "s")
-            if step >= 6 and (step - 6) % 4 == 0 and (step - 6) // 4 < EARLY:
-                turn_x((step - 6) // 4, "ss")
-            if step >= 4 and step % 2 == 0 and (step - 4) // 2 < RUNS // 2:
-                quantise_runs((step - 4) // 2)
-            if step >= 8 and (step - 8) % 4 == 0 and (step - 8) // 4 < EARLY:
-                quantise_x((step - 8) // 4)
-            if step == 1:
+                turn_run(*runs[step - 1])
+            m = step // 4 - 1
+            if step % 4 in (1, 2) and m >= 0:
+                quantise_part(m, step % 4 - 1)
+            if step % 4 in (1, 2) and 0 <= m < EARLY:
+                turn_x(m, step % 4 - 1, "s")
+            if step % 4 == 0 and 1 <= m <= EARLY:
+                quantise_x(m - 1)
+            if step == 3:
                 for n in range(4):
                     bps = psum.tile([P, 512], F32, tag="bank")
                     nc.tensor.matmul(bps[:], lhsT=ones[:], rhs=bz[:, 512 * n : 512 * n + 512], start=True, stop=True)
-                    nc.scalar.copy(out=bias_bc[:, 512 * n : 512 * n + 512], in_=bps[:])
-
-        by_s = [(mt, b) for mt in S_TILES for b in range(4)]
-        by_v = [(mt, b) for mt in range(MT) if mt not in S_TILES for b in range(4)]
+                    nc.vector.tensor_copy(out=bias_bc[:, 512 * n : 512 * n + 512], in_=bps[:])
         o_of = {}
 
-        def product(mt, b, by_scalar):
-            if b == 0:
-                o_sb = outp.tile([P, O], F32, tag="o_sb")
-                o_of[mt] = o_sb
-            evict(sums(mt, b), o_of[mt], b, by_scalar)
-            if b < 3:
-                return
-            o_sb = o_of[mt]
-            if not by_scalar:
-                nc.sync.dma_start(out=out[mt * P : (mt + 1) * P, :], in_=o_sb[:])
-                return
-            for half in range(2):
-                o_half = o_sb[:, 1024 * half : 1024 * half + 1024]
-                nc.gpsimd.tensor_tensor(out=o_half, in0=o_half, in1=bias_bc[:, 1024 * half : 1024 * half + 1024], op=ADD)
+        def o_tile(mt):
+            o_sb = outp.tile([P, O + 256], F32, tag="o_sb")
+            o_of[mt] = o_sb
 
-        def store_s(mt):
-            for half in range(2):
-                lo = 1024 * half
-                nc.sync.dma_start(out=out[mt * P : (mt + 1) * P, lo : lo + 1024], in_=o_of[mt][:, lo : lo + 1024])
+        def store(mt, lo, hi):
+            nc.sync.dma_start(out=out[mt * P : (mt + 1) * P, lo:hi], in_=o_of[mt][:, lo:hi])
 
-        for n in range(len(by_v)):
-            if n < len(by_s):
-                product(*by_s[n], True)
-            product(*by_v[n], False)
-            if n in (1, 3, 6, 8):
-                mt = {1: 4, 3: 5, 6: 6, 8: 7}[n]
-                turn_x(mt, "ss")
-                quantise_x(mt)
-            if n % 4 == 3 and 1 <= n // 4 <= len(S_TILES):
-                store_s(S_TILES[n // 4 - 1])
+        o_tile(0)
+        for mt in range(1, MT):
+            o_tile(mt)
+            for c in range(4):
+                if mt == 1:
+                    evict(sums(0, c), o_of[0], c, 0, 8, True)
+                acc = sums(mt, c)
+                if c == 2 and mt + 2 < MT:
+                    quantise_x(mt + 2)
+                evict(acc, o_of[mt], c, 0, 8, False)
+                if c == 0 and mt + 2 < MT:
+                    turn_x(mt + 2, 0, "s")
+                    turn_x(mt + 2, 1, "s")
+            if mt == 1:
+                for lo in range(0, O, 256):
+                    piece = o_of[0][:, lo : lo + 256]
+                    nc.gpsimd.tensor_tensor(out=piece, in0=piece, in1=bias_bc[:, lo : lo + 256], op=ADD)
+            store(mt, 0, O)
+            if mt == 3:
+                store(0, 0, O)

@@ -20,6 +20,7 @@ BYTES = M * K * 2 + M * O * 4 + 2 * O * 64 * 2 + O * 2
 EARLY = 3
 
 RUNS = 16
+AHEAD = 6
 GROUPS = [[t for t in range(RUNS) if 5 * t // 4 % 4 == c] for c in range(4)]
 WIN = 640
 ZWIN = 1024
@@ -47,6 +48,36 @@ def tile_structuredconnection_kernel(tc, x, weight, bias, mask, out):
         bz = keep.tile([P, O], BF16)
         bias_bc = keep.tile([P, O + 256], F32)
 
+        wt = weight.rearrange("(j t a) k -> t a j k", j=8, t=RUNS)
+        mk = mask.rearrange("(j t a) k -> t a j k", j=8, t=RUNS)
+
+        loaded = {}
+        order = [t for group in GROUPS for t in group]
+
+        def load_run(n):
+            t = order[n]
+            col = (640 * t) % K
+            first = min(WIN, K - col)
+            tiles = []
+            mask_queue = nc.gpsimd if n % 2 == 0 else nc.scalar
+            for queue, src, name in ((nc.sync, wt, "w_run"), (mask_queue, mk, "m_run")):
+                tile = wp.tile([P, WIN], BF16, tag=name, name=name)
+                queue.dma_start(out=tile[:, 0:first], in_=src[t, :, :, col : col + first])
+                if first < WIN:
+                    queue.dma_start(out=tile[:, first:WIN], in_=src[t, :, :, 0 : WIN - first])
+                tiles.append(tile)
+            loaded[t] = tiles
+
+        def load_x(mt):
+            nc.sync.dma_start(out=x_sb[:, mt, :], in_=x[mt * P : (mt + 1) * P, :])
+
+        def load(n):
+            load_run(n)
+            if n % 4 == 3:
+                load_x(n // 4)
+
+        load(0)
+        load(1)
         make_identity(nc, ident[:])
         nc.gpsimd.memset(bz[:].bitcast(F32), 0.0)
         nc.gpsimd.dma_start(out=bz[0:1, :], in_=bias.rearrange("(o n) -> o n", o=1))
@@ -55,25 +86,8 @@ def tile_structuredconnection_kernel(tc, x, weight, bias, mask, out):
         nc.scalar.copy(out=first[:], in_=first[:])
         nc.gpsimd.memset(ones[:], 1.0)
 
-        wt = weight.rearrange("(j t a) k -> t a j k", j=8, t=RUNS)
-        mk = mask.rearrange("(j t a) k -> t a j k", j=8, t=RUNS)
-
-        loaded = {}
-
-        def load_run(t):
-            col = (640 * t) % K
-            first = min(WIN, K - col)
-            tiles = []
-            for src, name in ((wt, "w_run"), (mk, "m_run")):
-                tile = wp.tile([P, WIN], BF16, tag=name, name=name)
-                nc.sync.dma_start(out=tile[:, 0:first], in_=src[t, :, :, col : col + first])
-                if first < WIN:
-                    nc.sync.dma_start(out=tile[:, first:WIN], in_=src[t, :, :, 0 : WIN - first])
-                tiles.append(tile)
-            loaded[t] = tiles
-
-        def load_x(mt):
-            nc.sync.dma_start(out=x_sb[:, mt, :], in_=x[mt * P : (mt + 1) * P, :])
+        for n in range(2, AHEAD):
+            load(n)
 
         zf = zt[:].rearrange("p t w -> p (t w)").bitcast(F32)
         zi = zt[:].rearrange("p t w -> p (t w)").bitcast(I32).rearrange("p (t w) -> p t w", t=RUNS)
@@ -177,30 +191,29 @@ def tile_structuredconnection_kernel(tc, x, weight, bias, mask, out):
                 i0 = i1
 
         runs = [(c, i) for c in range(4) for i in range(4)]
-        for c, i in runs:
-            load_run(GROUPS[c][i])
-            if i == 3:
-                load_x(c)
-        for mt in range(4, MT):
-            load_x(mt)
-        for step in range(RUNS + 5):
+        for step in range(RUNS + 4):
+            if step + AHEAD < RUNS:
+                load(step + AHEAD)
+            elif step + AHEAD < RUNS + 4:
+                load_x(step + AHEAD - RUNS + 4)
             if step < RUNS:
                 c, i = runs[step]
                 multiply(GROUPS[c][i])
-            if 1 <= step <= RUNS:
-                turn_run(*runs[step - 1])
-            m = step // 4 - 1
-            if step % 4 in (1, 2) and m >= 0:
-                quantise_part(m, step % 4 - 1)
-            if step % 4 in (1, 2) and 0 <= m < EARLY:
-                turn_x(m, step % 4 - 1, "s")
-            if step % 4 == 0 and 1 <= m <= EARLY:
-                quantise_x(m - 1)
-            if step == 3:
+            if 2 <= step < RUNS + 2:
+                turn_run(*runs[step - 2])
+            k, s = divmod(step - 6, 4)
+            if k >= 0 and s < 2:
+                quantise_part(k, s)
+                if k < EARLY:
+                    turn_x(k, s, "s")
+            if k >= 0 and s == 3 and k < EARLY:
+                quantise_x(k)
+            if step == 4:
                 for n in range(4):
                     bps = psum.tile([P, 512], F32, tag="bank")
                     nc.tensor.matmul(bps[:], lhsT=ones[:], rhs=bz[:, 512 * n : 512 * n + 512], start=True, stop=True)
                     nc.vector.tensor_copy(out=bias_bc[:, 512 * n : 512 * n + 512], in_=bps[:])
+
         o_of = {}
 
         def o_tile(mt):

from contextlib import ExitStack

import concourse.mybir as mybir
from concourse.masks import make_identity

F32 = mybir.dt.float32
BF16 = mybir.dt.bfloat16
U32 = mybir.dt.uint32
U8 = mybir.dt.uint8
I32 = mybir.dt.int32
FP8X4 = mybir.dt.float8_e4m3fn_x4
ADD = mybir.AluOpType.add
MULT = mybir.AluOpType.mult

P = 128
M, K, O = 1024, 2048, 2048
MT = M // P
FLOPS = 2 * M * O * 64
BYTES = M * K * 2 + M * O * 4 + 2 * O * 64 * 2 + O * 2
EARLY = 3

RUNS = 16
AHEAD = 6
GROUPS = [[t for t in range(RUNS) if 5 * t // 4 % 4 == c] for c in range(4)]
WIN = 640
ZWIN = 1024


def tile_structuredconnection_kernel(tc, x, weight, bias, mask, out):
    nc = tc.nc
    with ExitStack() as ctx:
        keep = ctx.enter_context(tc.tile_pool(name="keep", bufs=1))
        wp = ctx.enter_context(tc.tile_pool(name="wp", bufs=8))
        gp = ctx.enter_context(tc.tile_pool(name="gp", bufs=4))
        gwp = ctx.enter_context(tc.tile_pool(name="gwp", bufs=2))
        outp = ctx.enter_context(tc.tile_pool(name="outp", bufs=6))
        psum = ctx.enter_context(tc.psum_pool(name="psum", bufs=8))
        ctx.enter_context(tc.manual_schedule())

        zt = keep.tile([P, RUNS, ZWIN], BF16, align_bytes=64)
        wq = keep.tile([P, RUNS * 256], U32, align_bytes=64)
        ws = keep.tile([P, RUNS * 256], U8, align_bytes=64)
        x_sb = keep.tile([P, MT, K], BF16, align_bytes=64)
        xq = keep.tile([P, MT * 512], U32, align_bytes=64)
        xs = keep.tile([P, MT * 512], U8, align_bytes=64)
        ident = keep.tile([P, P], F32)
        ones = keep.tile([P, P], BF16)
        bz = keep.tile([P, O], BF16)
        bias_bc = keep.tile([P, O + 256], F32)

        wt = weight.rearrange("(j t a) k -> t a j k", j=8, t=RUNS)
        mk = mask.rearrange("(j t a) k -> t a j k", j=8, t=RUNS)

        loaded = {}
        order = [t for group in GROUPS for t in group]

        def load_run(n):
            t = order[n]
            col = (640 * t) % K
            first = min(WIN, K - col)
            tiles = []
            mask_queue = nc.gpsimd if n % 2 == 0 else nc.scalar
            for queue, src, name in ((nc.sync, wt, "w_run"), (mask_queue, mk, "m_run")):
                tile = wp.tile([P, WIN], BF16, tag=name, name=name)
                queue.dma_start(out=tile[:, 0:first], in_=src[t, :, :, col : col + first])
                if first < WIN:
                    queue.dma_start(out=tile[:, first:WIN], in_=src[t, :, :, 0 : WIN - first])
                tiles.append(tile)
            loaded[t] = tiles

        def load_x(mt):
            nc.sync.dma_start(out=x_sb[:, mt, :], in_=x[mt * P : (mt + 1) * P, :])

        def load(n):
            load_run(n)
            if n % 4 == 3:
                load_x(n // 4)

        load(0)
        load(1)
        make_identity(nc, ident[:])
        nc.gpsimd.memset(bz[:].bitcast(F32), 0.0)
        nc.gpsimd.dma_start(out=bz[0:1, :], in_=bias.rearrange("(o n) -> o n", o=1))
        first = keep.tile([P, 1], F32)
        nc.vector.memset(first[:], 0.0)
        nc.scalar.copy(out=first[:], in_=first[:])
        nc.gpsimd.memset(ones[:], 1.0)

        for n in range(2, AHEAD):
            load(n)

        zf = zt[:].rearrange("p t w -> p (t w)").bitcast(F32)
        zi = zt[:].rearrange("p t w -> p (t w)").bitcast(I32).rearrange("p (t w) -> p t w", t=RUNS)
        xf = x_sb[:].rearrange("p t k -> p (t k)").bitcast(F32)

        for r in range(4):
            if r > 0:
                nc.vector.memset(zi[:, r:RUNS:4, 0 : 64 * r], 0)
            if r < 3:
                nc.vector.memset(zi[:, r:RUNS:4, 64 * r + WIN // 2 : ZWIN // 2], 0)

        def copy_out(engine, dst, src):
            if engine == "s":
                nc.scalar.copy(out=dst, in_=src)
            else:
                nc.vector.tensor_copy(out=dst, in_=src)

        def multiply(t):
            d0 = 128 * (t % 4)
            w_run, m_run = loaded[t]
            nc.vector.tensor_tensor(out=zt[:, t, d0 : d0 + WIN], in0=w_run[:], in1=m_run[:], op=MULT)

        g_of = {}

        def turn_run(c, i):
            t = GROUPS[c][i]
            if i == 0:
                g = gwp.tile([P, 4096], BF16, align_bytes=64, tag="gw")
                g_of[c] = g
            gf = g_of[c][:].bitcast(F32).rearrange("p (b i j a u) -> p b i j a u", b=2, i=4, j=8, u=2)
            pt = psum.tile([P, 4, P], F32, tag="bank")
            for k in range(4):
                w0 = t * (ZWIN // 2) + P * k
                nc.tensor.transpose(pt[:, k, :], zf[:, w0 : w0 + P], ident[:])
            src = pt[:].rearrange("p (b u) (a j) -> p b j a u", b=2, j=8)
            for b in range(2):
                nc.scalar.copy(out=gf[:, b, i], in_=src[:, b])

        def quantise_part(c, b):
            lo = 1024 * c + 512 * b
            nc.vector.quantize_mx(
                out=wq[:, lo : lo + 512].bitcast(FP8X4),
                scales=ws[:, lo : lo + 512],
                in_=g_of[c][:, 2048 * b : 2048 * b + 2048],
            )

        xg_of = {}

        def turn_x(mt, h, engine):
            if h == 0:
                xg = gp.tile([P, 2048], BF16, align_bytes=64, tag="g")
                xg_of[mt] = xg
            xgf = xg_of[mt][:].bitcast(F32).rearrange("p (c m u) -> p c m u", c=4, u=2)
            pt = psum.tile([P, 4, P], F32, tag="bank")
            for k in range(4):
                w0 = mt * 1024 + 512 * h + P * k
                nc.tensor.transpose(pt[:, k, :], xf[:, w0 : w0 + P], ident[:])
            copy_out(engine, xgf[:, 2 * h : 2 * h + 2], pt[:].rearrange("p (c u) m -> p c m u", c=2))

        def quantise_x(mt):
            nc.vector.quantize_mx(
                out=xq[:, 512 * mt : 512 * mt + 512].bitcast(FP8X4),
                scales=xs[:, 512 * mt : 512 * mt + 512],
                in_=xg_of[mt][:],
            )

        def sums(mt, c):
            acc = psum.tile([P, 512], F32, tag="bank")
            for b in range(2):
                lo, xo = 1024 * c + 512 * b, 512 * mt + 128 * ((c + b) % 4)
                nc.tensor.matmul_mx(
                    out=acc[:],
                    lhsT=xq[:, xo : xo + 128].bitcast(FP8X4),
                    lhsT_scale=xs[:, xo : xo + 128],
                    rhs=wq[:, lo : lo + 512].bitcast(FP8X4),
                    rhs_scale=ws[:, lo : lo + 512],
                    start=(b == 0),
                    stop=(b == 1),
                )
            return acc

        def out_runs(t, b0, n):
            v = t[:, b0 : b0 + 2048].rearrange("p (j r) -> p j r", r=256)[:, :, 0 : 48 * n]
            return v.rearrange("p j (i e) -> p j i e", e=48)[:, :, :, 0:16]

        def evict(acc, o_sb, c, j0, j1, by_scalar):
            src = acc[:].rearrange("p (i j a) -> p j i a", i=4, j=8)
            i0 = 0
            while i0 < 4:
                i1 = i0 + 1
                while i1 < 4 and GROUPS[c][i1] == GROUPS[c][i1 - 1] + 3:
                    i1 += 1
                b0 = 16 * GROUPS[c][i0]
                dst, b = out_runs(o_sb, b0, i1 - i0), out_runs(bias_bc, b0, i1 - i0)
                if by_scalar:
                    nc.scalar.copy(out=dst[:, j0:j1], in_=src[:, j0:j1, i0:i1])
                else:
                    nc.vector.tensor_tensor(
                        out=dst[:, j0:j1], in0=src[:, j0:j1, i0:i1], in1=b[:, j0:j1], op=ADD
                    )
                i0 = i1

        runs = [(c, i) for c in range(4) for i in range(4)]
        for step in range(RUNS + 4):
            if step + AHEAD < RUNS:
                load(step + AHEAD)
            elif step + AHEAD < RUNS + 4:
                load_x(step + AHEAD - RUNS + 4)
            if step < RUNS:
                c, i = runs[step]
                multiply(GROUPS[c][i])
            if 2 <= step < RUNS + 2:
                turn_run(*runs[step - 2])
            k, s = divmod(step - 6, 4)
            if k >= 0 and s < 2:
                quantise_part(k, s)
                if k < EARLY:
                    turn_x(k, s, "s")
            if k >= 0 and s == 3 and k < EARLY:
                quantise_x(k)
            if step == 4:
                for n in range(4):
                    bps = psum.tile([P, 512], F32, tag="bank")
                    nc.tensor.matmul(bps[:], lhsT=ones[:], rhs=bz[:, 512 * n : 512 * n + 512], start=True, stop=True)
                    nc.vector.tensor_copy(out=bias_bc[:, 512 * n : 512 * n + 512], in_=bps[:])

        o_of = {}

        def o_tile(mt):
            o_sb = outp.tile([P, O + 256], F32, tag="o_sb")
            o_of[mt] = o_sb

        def store(mt, lo, hi):
            nc.sync.dma_start(out=out[mt * P : (mt + 1) * P, lo:hi], in_=o_of[mt][:, lo:hi])

        o_tile(0)
        for mt in range(1, MT):
            o_tile(mt)
            for c in range(4):
                if mt == 1:
                    evict(sums(0, c), o_of[0], c, 0, 8, True)
                acc = sums(mt, c)
                if c == 2 and mt + 2 < MT:
                    quantise_x(mt + 2)
                evict(acc, o_of[mt], c, 0, 8, False)
                if c == 0 and mt + 2 < MT:
                    turn_x(mt + 2, 0, "s")
                    turn_x(mt + 2, 1, "s")
            if mt == 1:
                for lo in range(0, O, 256):
                    piece = o_of[0][:, lo : lo + 256]
                    nc.gpsimd.tensor_tensor(out=piece, in0=piece, in1=bias_bc[:, lo : lo + 256], op=ADD)
            store(mt, 0, O)
            if mt == 3:
                store(0, 0, O)
